import numpy as np
import ml_dtypes


def mxq(x, axis, fmt="e4m3"):
    dtype, down = {"e4m3": (ml_dtypes.float8_e4m3fn, 7), "e5m2": (ml_dtypes.float8_e5m2, 14)}[fmt]
    v = np.moveaxis(np.asarray(x, np.float32).astype(ml_dtypes.bfloat16).astype(np.float64), axis, -1)
    blocks = v.reshape(v.shape[:-1] + (-1, 32))
    amax = np.abs(blocks).max(-1, keepdims=True)
    byte = np.maximum(np.where(amax > 0, np.frexp(amax)[1] - 1 + 127, 0) - down, 1)
    scale = np.exp2(byte - 127.0)
    codes = (blocks / scale).astype(np.float32).astype(dtype).astype(np.float64)
    return np.moveaxis((codes * scale).reshape(v.shape), -1, axis)


WIDE = False


def mx_kscale(k):
    if not WIDE:
        return np.ones(k)
    levels = np.array([18, -18])
    if k % 512:
        return np.exp2(np.random.permutation(np.resize(levels, k // 32))).repeat(32)
    a = np.empty((k // 512, 16))
    for p in range(k // 512):
        a[p, :8] = np.random.permutation(np.resize(levels, 8))
        for g in range(8):
            far = levels[np.abs(levels - a[p, g]) >= 10]
            a[p, g + 8] = far[np.random.randint(len(far))]
    return np.exp2(a.ravel()).repeat(32)


BF16 = ml_dtypes.bfloat16


def bf(x):
    return np.asarray(x, np.float32).astype(BF16)


def f64(x):
    return np.asarray(x).astype(np.float64)


B, S, D = 128, 16, 512
T = B * S


def sigmoid(v):
    return 1.0 / (1.0 + np.exp(-v))


def gate_sums(inputs, h_state, kernel, recurrent_kernel, bias):
    xz = f64(inputs) @ f64(kernel)
    hz = f64(h_state).reshape(B, S, D) @ f64(recurrent_kernel)
    return xz[:, None, :] + hz + f64(bias)


def setup_inputs():
    s = mx_kscale(T).reshape(B, S, 1)
    u = mx_kscale(D)
    inputs = bf(np.random.standard_normal((B, D)))
    h0 = bf((np.random.standard_normal((B, S, D)) * 0.5).reshape(B, S * D))
    c_state = bf(np.random.standard_normal((B, S * D)) * 0.5)
    c_upd = bf(np.random.standard_normal((B, S, D)))
    kernel = bf(np.random.standard_normal((D, 3 * D)) / np.sqrt(D))
    r0 = bf(np.random.standard_normal((D, 3 * D)) / np.sqrt(D))
    bias = bf(np.random.standard_normal(3 * D) * 0.3)
    z = gate_sums(inputs, h0, kernel, r0, bias)
    g0 = np.random.standard_normal((B, S, D)) * np.exp2(np.random.randint(-6, 1, (B, S, 1))) * 4.0
    g1 = np.random.standard_normal((B, S, D)) * np.exp2(np.random.randint(-6, 1, (B, S, 1))) * 4.0
    return {
        "inputs": inputs,
        "h_state": bf((f64(h0).reshape(B, S, D) * s).reshape(B, S * D)),
        "c_state": c_state,
        "c_upd": c_upd,
        "kernel": kernel,
        "recurrent_kernel": bf(f64(r0) / np.tile(u, 3)),
        "bias": bias,
        "z": np.asarray(z, np.float32),
        "grad_0": bf((g0 / s * u).reshape(B, S * D)),
        "grad_1": bf((g1 / s * u).reshape(B, S * D)),
    }


def reference(inputs, h_state, c_state, c_upd, kernel, recurrent_kernel, bias, z, grad_0, grad_1):
    h = f64(h_state).reshape(T, D)
    c = f64(c_state).reshape(T, D)
    a = np.tanh(f64(c_upd).reshape(T, D))
    zf = f64(z).reshape(T, 3 * D)
    g0 = f64(grad_0).reshape(T, D)
    g1 = f64(grad_1).reshape(T, D)
    i = sigmoid(zf[:, :D])
    f = sigmoid(zf[:, D:2 * D])
    o = sigmoid(zf[:, 2 * D:])
    tc = np.tanh(f * c + i * a)
    dc = g1 + g0 * o * (1.0 - tc * tc)
    dzi = dc * a * i * (1.0 - i)
    dzf = dc * c * f * (1.0 - f)
    dzo = g0 * tc * o * (1.0 - o)
    dz = np.concatenate([dzi, dzf, dzo], axis=1)
    dh = mxq(dz, 1, "e5m2") @ mxq(f64(recurrent_kernel), 1, "e4m3").T
    dr = mxq(h, 0, "e4m3").T @ mxq(dz, 0, "e5m2")
    return dh.reshape(B, S * D), dr

@@ -1,0 +1,367 @@
+from contextlib import ExitStack
+
+import concourse.mybir as mybir
+from concourse.masks import make_identity
+
+T, D = 2048, 512
+FLOPS = 2 * 2 * T * D * 3 * D
+BYTES = T * 3 * D * 4 + 5 * T * D * 2 + D * 3 * D * 2 + T * D * 4 + D * 3 * D * 4
+
+F32 = mybir.dt.float32
+BF16 = mybir.dt.bfloat16
+U32 = mybir.dt.uint32
+U8 = mybir.dt.uint8
+E4 = mybir.dt.float8_e4m3fn_x4
+E5 = mybir.dt.float8_e5m2_x4
+ACT = mybir.ActivationFunctionType
+ALU = mybir.AluOpType
+
+P = 128
+GROUPS = 4
+HALF = 256
+STEPS = 8
+PASS_O = 2
+CN_BANKS = (0, 1)
+TC_BANKS = (2, 0)
+SQ_BANKS = (3, 1)
+DZT_BANKS = (4, 5)
+ACC_BANKS = (6, 7)
+
+
+def tile_rlstmcell_pb_v_kernel(tc, inputs, h_state, c_state, c_upd, kernel, recurrent_kernel, bias,
+                                            z, grad_0, grad_1, out_0, out_1):
+    nc = tc.nc
+
+    def by_token(ap):
+        return ap.rearrange("b (s d) -> (b s) d", d=D).rearrange("(g p j) d -> g p j d", p=P, j=4)
+
+    h_hbm, c_hbm, g0_hbm, g1_hbm, dh_hbm = (by_token(ap) for ap in (h_state, c_state, grad_0, grad_1, out_0))
+    cu_hbm = c_upd.rearrange("b s d -> (b s) d").rearrange("(g p j) d -> g p j d", p=P, j=4)
+    z_hbm = z.rearrange("b s k -> (b s) k").rearrange("(g p j) k -> g p j k", p=P, j=4)
+    r_hbm = recurrent_kernel.rearrange("(a p) k -> p a k", p=P)
+    dr_hbm = out_1.rearrange("(a p) (gate c) -> a p gate c", p=P, gate=3)
+
+    with ExitStack() as ctx:
+        keep = ctx.enter_context(tc.tile_pool(name="keep", bufs=1))
+        two = ctx.enter_context(tc.tile_pool(name="two", bufs=2))
+        three = ctx.enter_context(tc.tile_pool(name="three", bufs=3))
+        psum = ctx.enter_context(tc.psum_pool(name="psum", bufs=1))
+
+        ident = keep.tile([P, P], F32, name="ident")
+        make_identity(nc, ident[:])
+        warm = keep.tile([P, 8], F32, name="warm")
+
+        def bank(k):
+            return psum.tile([P, 512], F32, name="bank%d" % k, tag="bank%d" % k)
+
+        def quantised(pool, name):
+            codes = pool.tile([P, 512], U32, name=name + "_codes", tag=name + "_codes", align_bytes=64)
+            scales = pool.tile([P, 512], U8, name=name + "_scales", tag=name + "_scales", align_bytes=64)
+            return codes, scales
+
+        def quantise(pool, name, src, fmt):
+            codes, scales = quantised(pool, name)
+            nc.vector.quantize_mx(out=codes[:].bitcast(fmt), scales=scales[:], in_=src[:])
+            return codes, scales
+
+        def mx(out, lhs, lhs_fmt, col, rhs, rhs_fmt, start, stop):
+            cols = slice(P * col, P * (col + 1))
+            nc.tensor.matmul_mx(out=out[:], lhsT=lhs[0][:, cols].bitcast(lhs_fmt), lhsT_scale=lhs[1][:, cols],
+                                rhs=rhs[0][:].bitcast(rhs_fmt), rhs_scale=rhs[1][:], start=start, stop=stop)
+
+        st = [dict() for n in range(STEPS)]
+        dz_o = [keep.tile([P, 2048], BF16, name="dz_o%d" % g, align_bytes=64) for g in range(GROUPS)]
+        tok_q, feat_q, h_q, r_q, h_raw, r_raw, grouped = {}, {}, {}, {}, {}, {}, {}
+
+        def load_step(n):
+            half, g = divmod(n, GROUPS)
+            cols = slice(HALF * half, HALF * (half + 1))
+            for name, src, gate in (("cu", cu_hbm, 0), ("i", z_hbm, 0), ("c", c_hbm, 0), ("f", z_hbm, 1),
+                                    ("g0", g0_hbm, 0), ("o", z_hbm, 2), ("g1", g1_hbm, 0)):
+                dtype = F32 if src is z_hbm else BF16
+                t = three.tile([P, 4, HALF], dtype, name=name, tag=name)
+                nc.sync.dma_start(out=t[:], in_=src[g][:, :, D * gate + cols.start:D * gate + cols.stop])
+                st[n][name] = t
+
+        def load_h(g):
+            h_raw[g] = two.tile([P, 4, D], BF16, name="h_raw", tag="h_raw")
+            nc.sync.dma_start(out=h_raw[g][:], in_=h_hbm[g])
+
+        def load_r(s):
+            r_raw[s] = three.tile([P, 4, D], BF16, name="r_raw", tag="out_stage")
+            if s == PASS_O:
+                nc.sync.dma_start(out=r_raw[s][:], in_=r_hbm[:, :, 2 * D:3 * D])
+            else:
+                for gate in range(2):
+                    first = D * gate + HALF * s
+                    nc.sync.dma_start(out=r_raw[s][:, :, HALF * gate:HALF * (gate + 1)],
+                                      in_=r_hbm[:, :, first:first + HALF])
+
+        def tanh_a(n):
+            st[n]["a"] = three.tile([P, 4, HALF], F32, name="a", tag="a")
+            nc.scalar.activation(out=st[n]["a"][:], in_=st[n]["cu"][:], func=ACT.Tanh)
+
+        def sigmoid(n, gate):
+            nc.scalar.activation(out=st[n][gate][:], in_=st[n][gate][:], func=ACT.Sigmoid)
+
+        def cell_terms(n):
+            s = st[n]
+            nc.vector.tensor_tensor(out=s["a"][:], in0=s["i"][:], in1=s["a"][:], op=ALU.mult)
+            s["fc"] = two.tile([P, 4, HALF], F32, name="fc", tag="fc")
+            nc.vector.tensor_tensor(out=s["fc"][:], in0=s["f"][:], in1=s["c"][:], op=ALU.mult)
+
+        def g0_times_o(n):
+            s = st[n]
+            s["g0o"] = two.tile([P, 4, HALF], F32, name="g0o", tag="g0o")
+            nc.vector.tensor_tensor(out=s["g0o"][:], in0=s["o"][:], in1=s["g0"][:], op=ALU.mult)
+
+        def minus_one_times(out, gate, other):
+            nc.vector.scalar_tensor_tensor(out=out, in0=gate, scalar=1.0, in1=other, op0=ALU.subtract, op1=ALU.mult)
+
+        def gate_slopes(n):
+            s = st[n]
+            minus_one_times(s["fc"][:], s["f"][:], s["fc"][:])
+            minus_one_times(s["o"][:], s["o"][:], s["g0o"][:])
+            minus_one_times(s["a"][:], s["i"][:], s["a"][:])
+
+        def new_cell_transposed(n):
+            s = st[n]
+            s["cn"] = []
+            for q in range(2):
+                b = bank(CN_BANKS[q])
+                for j in range(4):
+                    for k, term in enumerate(("a", "fc")):
+                        nc.tensor.matmul(out=b[:, P * j:P * (j + 1)], lhsT=s[term][:, j, P * q:P * (q + 1)],
+                                         rhs=ident[:], start=(k == 0), stop=(k == 1), is_transpose=True)
+                s["cn"].append(b)
+
+        def tanh_and_square(n):
+            s = st[n]
+            s["ntc"] = [two.tile([P, 512], F32, name="ntc", tag="ntc") for q in range(2)]
+            s["sq"] = [two.tile([P, 512], F32, name="sq", tag="sq") for q in range(2)]
+            for q in range(2):
+                nc.scalar.activation(out=s["ntc"][q][:], in_=s["cn"][q][:], func=ACT.Tanh, scale=-1.0)
+            for q in range(2):
+                nc.scalar.activation(out=s["sq"][q][:], in_=s["ntc"][q][:], func=ACT.Square)
+
+        def transpose_back(n):
+            s = st[n]
+            for name, banks in (("ntc", TC_BANKS), ("sq", SQ_BANKS)):
+                s[name + "_ps"] = []
+                for q in range(2):
+                    b = bank(banks[q])
+                    for j in range(4):
+                        nc.tensor.transpose(b[:, P * j:P * (j + 1)], s[name][q][:, P * j:P * (j + 1)], ident[:])
+                    s[name + "_ps"].append(b)
+
+        def rounded_product(dz, first, count, in0, in1):
+            out = dz[:].rearrange("p (t m j) -> p m j t", t=4, j=4)[:, first:first + count]
+            nc.vector.tensor_tensor(out=out, in0=in0.rearrange("p j (m t) -> p m j t", t=4),
+                                    in1=in1.rearrange("p j (m t) -> p m j t", t=4), op=ALU.mult)
+
+        def psum_products(n, q):
+            half, g = divmod(n, GROUPS)
+            s = st[n]
+            cols = slice(P * q, P * (q + 1))
+            minus_one_times(s["g0o"][:, :, cols], s["sq_ps"][q][:].rearrange("p (j c) -> p j c", j=4),
+                            s["g0o"][:, :, cols])
+            rounded_product(dz_o[g], 64 * half + 32 * q, 32, s["ntc_ps"][q][:].rearrange("p (j c) -> p j c", j=4),
+                            s["o"][:, :, cols])
+
+        def minus_dc(n):
+            s = st[n]
+            nc.vector.tensor_tensor(out=s["g0o"][:], in0=s["g0o"][:], in1=s["g1"][:], op=ALU.subtract)
+
+        def dz_i_and_f(n):
+            s = st[n]
+            s["dz"] = two.tile([P, 2048], BF16, name="dz_if", tag="dz_if", align_bytes=64)
+            rounded_product(s["dz"], 0, 64, s["a"][:], s["g0o"][:])
+            rounded_product(s["dz"], 64, 64, s["fc"][:], s["g0o"][:])
+
+        def transpose_dz(dz):
+            words = dz[:].bitcast(F32)
+            banks = []
+            for u in range(2):
+                b = bank(DZT_BANKS[u])
+                for t in range(4):
+                    nc.tensor.transpose(b[:, P * t:P * (t + 1)], words[:, 256 * t + u:256 * (t + 1):2], ident[:])
+                banks.append(b)
+            return banks
+
+        def group_features(key, tag, banks, second_engine_copy):
+            grouped[key] = two.tile([P, 2048], BF16, name=tag, tag=tag, align_bytes=64)
+            for u, copy in enumerate((nc.scalar.copy, second_engine_copy)):
+                out = grouped[key][:, 1024 * u:1024 * (u + 1)].rearrange("m (e p t) -> m e p t", e=2, t=4)
+                copy(out=out, in_=banks[u][:].bitcast(BF16).rearrange("m (t p e) -> m e p t", t=4, e=2))
+
+        def group_h(g):
+            grouped["h", g] = two.tile([P, 2048], BF16, name="stage_o", tag="stage_o", align_bytes=64)
+            nc.scalar.copy(out=grouped["h", g][:].rearrange("p (c i j) -> p c j i", i=4, j=4),
+                           in_=h_raw[g][:].rearrange("p j (c i) -> p c j i", i=4))
+
+        def transpose_r(s):
+            words = r_raw[s][:].rearrange("p a k -> p (a k)").bitcast(F32)
+            banks = []
+            for pair in range(2):
+                b = bank(ACC_BANKS[pair])
+                for a in range(2):
+                    for u in range(2):
+                        first = 256 * (2 * pair + a)
+                        nc.tensor.transpose(b[:, P * (2 * a + u):P * (2 * a + u + 1)],
+                                            words[:, first + u:first + 256:2], ident[:])
+                banks.append(b)
+            return banks
+
+        def group_r(s, banks):
+            grouped["r", s] = keep.tile([P, 2048], BF16, name="stage_r", tag="stage_r", align_bytes=64)
+            words = grouped["r", s][:].bitcast(F32)
+            for pair in range(2):
+                nc.scalar.copy(out=words[:, 512 * pair:512 * (pair + 1)].rearrange("m (a d u) -> m a d u", a=2, u=2),
+                               in_=banks[pair][:].rearrange("m (a u d) -> m a d u", a=2, u=2))
+
+        def dh_tile(g, j, k):
+            b = bank(k)
+            for place, s in enumerate((0, PASS_O, 1)):
+                mx(b, feat_q[g, s], E5, j, r_q[s], E4, place == 0, place == 2)
+            return b
+
+        def dh_pair(g, pair, banks):
+            return [dh_tile(g, 2 * pair + e, banks[e]) for e in range(2)]
+
+        def store_dh_pair(g, pair, banks, second_engine_copy):
+            stage = three.tile([P, 2, D], F32, name="dh_stage", tag="out_stage")
+            for e, copy in enumerate((nc.scalar.copy, second_engine_copy)):
+                copy(out=stage[:, e, :], in_=banks[e][:])
+            nc.sync.dma_start(out=dh_hbm[g][:, 2 * pair:2 * pair + 2, :], in_=stage[:])
+
+        def dr_tile(s, a, k):
+            b = bank(k)
+            for g in range(GROUPS):
+                mx(b, h_q[g], E4, a, tok_q[g, s], E5, g == 0, g == GROUPS - 1)
+            return b
+
+        def store_dr_tile(s, a, b, copy, tag):
+            stage = three.tile([P, D], F32, name="dr_stage", tag=tag)
+            copy(out=stage[:].rearrange("p (m t) -> p m t", t=4), in_=b[:].rearrange("p (t m) -> p m t", t=4))
+            if s == PASS_O:
+                nc.sync.dma_start(out=dr_hbm[a][:, 2, :], in_=stage[:])
+            else:
+                nc.sync.dma_start(out=dr_hbm[a][:, 0:2, HALF * s:HALF * (s + 1)],
+                                  in_=stage[:].rearrange("p (gate c) -> p gate c", gate=2))
+
+        def quantise_features_if(n):
+            half, g = divmod(n, GROUPS)
+            pool, name = (keep, "feat0_%d" % g) if half == 0 else (two, "feat1")
+            feat_q[g, half] = quantise(pool, name, grouped["if", n], E5)
+
+        s_copy, v_copy = nc.scalar.copy, nc.vector.tensor_copy
+
+        ctx.enter_context(tc.manual_schedule())
+        nc.scalar.activation(out=warm[:], in_=ident[:, 0:8], func=ACT.Sigmoid)
+        load_step(0)
+        load_step(1)
+        load_h(0)
+        load_r(0)
+        load_step(2)
+        load_h(1)
+        load_r(1)
+        load_r(2)
+        tanh_a(0)
+        for gate in ("i", "f", "o"):
+            sigmoid(0, gate)
+
+        late_dh = None
+        for n in range(-1, STEPS - 1):
+            half, g = divmod(n, GROUPS)
+            if n >= 0:
+                psum_products(n, 0)
+                psum_products(n, 1)
+            if late_dh is not None:
+                store_dh_pair(n - 2 - GROUPS, 1, late_dh, s_copy)
+                late_dh = None
+            if half == 1:
+                o_banks = transpose_dz(dz_o[g])
+            cell_terms(n + 1)
+            if half == 1:
+                group_features(("o", g), "stage_o", o_banks, s_copy)
+                dr_bank = dr_tile(0, g, TC_BANKS[0])
+            elif n >= 0:
+                group_h(g)
+                if g + 2 < GROUPS:
+                    load_h(g + 2)
+            if 0 <= n < 3:
+                r_banks = transpose_r(n)
+            new_cell_transposed(n + 1)
+            if n >= 0:
+                minus_dc(n)
+            g0_times_o(n + 1)
+            if n >= 0:
+                dz_i_and_f(n)
+            if n + 2 < STEPS:
+                tanh_a(n + 2)
+                sigmoid(n + 2, "i")
+            if 0 <= n and n + 3 < STEPS:
+                load_step(n + 3)
+            if half == 1:
+                store_dr_tile(0, g, dr_bank, s_copy, "out_stage")
+            if 0 <= n < 3:
+                group_r(n, r_banks)
+            tanh_and_square(n + 1)
+            if n >= 0:
+                if_banks = transpose_dz(st[n]["dz"])
+            if n >= 1:
+                quantise_features_if(n - 1)
+            if n >= 0:
+                tok_q[g, half] = quantise(keep, "tok%d_%d" % (g, half), st[n]["dz"], E5)
+            if half == 1:
+                tok_q[g, PASS_O] = quantise(keep, "tok%d_o" % g, dz_o[g], E5)
+                feat_q[g, PASS_O] = quantise(two, "feat_o", grouped["o", g], E5)
+            elif n >= 0:
+                h_q[g] = quantise(keep, "h%d" % g, grouped["h", g], E4)
+            if 0 <= n < 3:
+                r_q[n] = quantise(keep, "r%d" % n, grouped["r", n], E4)
+            if n > GROUPS:
+                early_dh = dh_pair(g - 1, 0, ACC_BANKS)
+            transpose_back(n + 1)
+            gate_slopes(n + 1)
+            if n + 2 < STEPS:
+                sigmoid(n + 2, "f")
+            if n > GROUPS:
+                store_dh_pair(g - 1, 0, early_dh, s_copy)
+                late_dh = dh_pair(g - 1, 1, ACC_BANKS)
+            if n + 2 < STEPS:
+                sigmoid(n + 2, "o")
+            if n >= 0:
+                group_features(("if", n), "stage_if", if_banks, s_copy)
+
+        n, g = STEPS - 1, GROUPS - 1
+        store_dh_pair(g - 2, 1, late_dh, s_copy)
+        psum_products(n, 0)
+        quantise_features_if(n - 1)
+        psum_products(n, 1)
+        early_dh = dh_pair(g - 1, 0, ACC_BANKS)
+        dr_bank = dr_tile(0, g, TC_BANKS[0])
+        store_dh_pair(g - 1, 0, early_dh, s_copy)
+        o_banks = transpose_dz(dz_o[g])
+        late_dh = dh_pair(g - 1, 1, ACC_BANKS)
+        minus_dc(n)
+        tok_q[g, PASS_O] = quantise(keep, "tok%d_o" % g, dz_o[g], E5)
+        dz_i_and_f(n)
+        store_dr_tile(0, g, dr_bank, s_copy, "i")
+        group_features(("o", g), "stage_o", o_banks, s_copy)
+        store_dh_pair(g - 1, 1, late_dh, s_copy)
+        o_tiles = [dr_tile(PASS_O, a, k) for a, k in enumerate((0, 1))]
+        if_banks = transpose_dz(st[n]["dz"])
+        o_tiles.extend([dr_tile(PASS_O, 2 + a, k) for a, k in enumerate((3, 2))])
+        tok_q[g, 1] = quantise(keep, "tok%d_1" % g, st[n]["dz"], E5)
+        feat_q[g, PASS_O] = quantise(two, "feat_o", grouped["o", g], E5)
+        group_features(("if", n), "stage_if", if_banks, v_copy)
+        store_dr_tile(PASS_O, 0, o_tiles[0], s_copy, "i")
+        store_dr_tile(PASS_O, 1, o_tiles[1], v_copy, "f")
+        quantise_features_if(n)
+        store_dr_tile(PASS_O, 2, o_tiles[2], s_copy, "i")
+        store_dr_tile(PASS_O, 3, o_tiles[3], v_copy, "f")
+        for pair, banks in enumerate((ACC_BANKS, DZT_BANKS)):
+            store_dh_pair(g, pair, dh_pair(g, pair, banks), v_copy)
+        for a in range(4):
+            store_dr_tile(1, a, dr_tile(1, a, a), (s_copy, v_copy)[a % 2], ("o", "a")[a % 2])

@@ -45,6 +45,7 @@ def tile_rlstmcell_pb_v_kernel(tc, inputs, h_state, c_state, c_upd, kernel, recu
         keep = ctx.enter_context(tc.tile_pool(name="keep", bufs=1))
         two = ctx.enter_context(tc.tile_pool(name="two", bufs=2))
         three = ctx.enter_context(tc.tile_pool(name="three", bufs=3))
+        four = ctx.enter_context(tc.tile_pool(name="four", bufs=4))
         psum = ctx.enter_context(tc.psum_pool(name="psum", bufs=1))
 
         ident = keep.tile([P, P], F32, name="ident")
@@ -79,7 +80,8 @@ def tile_rlstmcell_pb_v_kernel(tc, inputs, h_state, c_state, c_upd, kernel, recu
             for name, src, gate in (("cu", cu_hbm, 0), ("i", z_hbm, 0), ("c", c_hbm, 0), ("f", z_hbm, 1),
                                     ("g0", g0_hbm, 0), ("o", z_hbm, 2), ("g1", g1_hbm, 0)):
                 dtype = F32 if src is z_hbm else BF16
-                t = three.tile([P, 4, HALF], dtype, name=name, tag=name)
+                pool = four if name == "i" else three
+                t = pool.tile([P, 4, HALF], dtype, name=name, tag=name)
                 nc.sync.dma_start(out=t[:], in_=src[g][:, :, D * gate + cols.start:D * gate + cols.stop])
                 st[n][name] = t
 
@@ -104,16 +106,19 @@ def tile_rlstmcell_pb_v_kernel(tc, inputs, h_state, c_state, c_upd, kernel, recu
         def sigmoid(n, gate):
             nc.scalar.activation(out=st[n][gate][:], in_=st[n][gate][:], func=ACT.Sigmoid)
 
-        def cell_terms(n):
+        def i_times_a(n):
             s = st[n]
             nc.vector.tensor_tensor(out=s["a"][:], in0=s["i"][:], in1=s["a"][:], op=ALU.mult)
+
+        def f_times_c(n):
+            s = st[n]
             s["fc"] = two.tile([P, 4, HALF], F32, name="fc", tag="fc")
             nc.vector.tensor_tensor(out=s["fc"][:], in0=s["f"][:], in1=s["c"][:], op=ALU.mult)
 
-        def g0_times_o(n):
+        def g0_times_o(n, engine, out):
             s = st[n]
-            s["g0o"] = two.tile([P, 4, HALF], F32, name="g0o", tag="g0o")
-            nc.vector.tensor_tensor(out=s["g0o"][:], in0=s["o"][:], in1=s["g0"][:], op=ALU.mult)
+            s["g0o"] = out
+            engine.tensor_tensor(out=out[:], in0=s["o"][:], in1=s["g0"][:], op=ALU.mult)
 
         def minus_one_times(out, gate, other):
             nc.vector.scalar_tensor_tensor(out=out, in0=gate, scalar=1.0, in1=other, op0=ALU.subtract, op1=ALU.mult)
@@ -219,14 +224,15 @@ def tile_rlstmcell_pb_v_kernel(tc, inputs, h_state, c_state, c_upd, kernel, recu
                 nc.scalar.copy(out=words[:, 512 * pair:512 * (pair + 1)].rearrange("m (a d u) -> m a d u", a=2, u=2),
                                in_=banks[pair][:].rearrange("m (a u d) -> m a d u", a=2, u=2))
 
-        def dh_tile(g, j, k):
-            b = bank(k)
-            for place, s in enumerate((0, PASS_O, 1)):
-                mx(b, feat_q[g, s], E5, j, r_q[s], E4, place == 0, place == 2)
-            return b
+        def dh_passes(g, j, b, passes):
+            for s in passes:
+                mx(b, feat_q[g, s], E5, j, r_q[s], E4, s == 0, s == 1)
 
-        def dh_pair(g, pair, banks):
-            return [dh_tile(g, 2 * pair + e, banks[e]) for e in range(2)]
+        def dh_pair(g, pair, bank_numbers):
+            banks = [bank(k) for k in bank_numbers]
+            for e in range(2):
+                dh_passes(g, 2 * pair + e, banks[e], (0, PASS_O, 1))
+            return banks
 
         def store_dh_pair(g, pair, banks, second_engine_copy):
             stage = three.tile([P, 2, D], F32, name="dh_stage", tag="out_stage")
@@ -234,14 +240,17 @@ def tile_rlstmcell_pb_v_kernel(tc, inputs, h_state, c_state, c_upd, kernel, recu
                 copy(out=stage[:, e, :], in_=banks[e][:])
             nc.sync.dma_start(out=dh_hbm[g][:, 2 * pair:2 * pair + 2, :], in_=stage[:])
 
-        def dr_tile(s, a, k):
-            b = bank(k)
-            for g in range(GROUPS):
+        def dr_passes(s, a, b, groups):
+            for g in groups:
                 mx(b, h_q[g], E4, a, tok_q[g, s], E5, g == 0, g == GROUPS - 1)
+
+        def dr_tile(s, a, k, groups):
+            b = bank(k)
+            dr_passes(s, a, b, groups)
             return b
 
-        def store_dr_tile(s, a, b, copy, tag):
-            stage = three.tile([P, D], F32, name="dr_stage", tag=tag)
+        def store_dr_tile(s, a, b, copy, pool, tag):
+            stage = pool.tile([P, D], F32, name="dr_stage", tag=tag)
             copy(out=stage[:].rearrange("p (m t) -> p m t", t=4), in_=b[:].rearrange("p (t m) -> p m t", t=4))
             if s == PASS_O:
                 nc.sync.dma_start(out=dr_hbm[a][:, 2, :], in_=stage[:])
@@ -258,6 +267,7 @@ def tile_rlstmcell_pb_v_kernel(tc, inputs, h_state, c_state, c_upd, kernel, recu
 
         ctx.enter_context(tc.manual_schedule())
         nc.scalar.activation(out=warm[:], in_=ident[:, 0:8], func=ACT.Sigmoid)
+        first_g0o = four.tile([P, 4, HALF], F32, name="first_g0o", tag="i")
         load_step(0)
         load_step(1)
         load_h(0)
@@ -270,21 +280,31 @@ def tile_rlstmcell_pb_v_kernel(tc, inputs, h_state, c_state, c_upd, kernel, recu
         for gate in ("i", "f", "o"):
             sigmoid(0, gate)
 
+        all_groups, early_groups, last_group = range(GROUPS), range(GROUPS - 1), (GROUPS - 1,)
+        dr_plan = {4: (0, 1), 5: (2,), 6: (3,)}
         late_dh = None
         for n in range(-1, STEPS - 1):
             half, g = divmod(n, GROUPS)
             if n >= 0:
+                g0_times_o(n + 1, nc.gpsimd, st[n]["i"])
                 psum_products(n, 0)
                 psum_products(n, 1)
             if late_dh is not None:
-                store_dh_pair(n - 2 - GROUPS, 1, late_dh, s_copy)
+                store_dh_pair(n - 2 - GROUPS, 1, late_dh, v_copy)
                 late_dh = None
             if half == 1:
                 o_banks = transpose_dz(dz_o[g])
-            cell_terms(n + 1)
+            if n >= 1:
+                quantise_features_if(n - 1)
+            i_times_a(n + 1)
+            if n >= 0:
+                minus_dc(n)
+            f_times_c(n + 1)
+            if n > GROUPS:
+                early_dh = dh_pair(g - 1, 0, ACC_BANKS)
             if half == 1:
                 group_features(("o", g), "stage_o", o_banks, s_copy)
-                dr_bank = dr_tile(0, g, TC_BANKS[0])
+                dr_banks = [dr_tile(0, a, 2 + k, all_groups) for k, a in enumerate(dr_plan[n])]
             elif n >= 0:
                 group_h(g)
                 if g + 2 < GROUPS:
@@ -292,76 +312,80 @@ def tile_rlstmcell_pb_v_kernel(tc, inputs, h_state, c_state, c_upd, kernel, recu
             if 0 <= n < 3:
                 r_banks = transpose_r(n)
             new_cell_transposed(n + 1)
-            if n >= 0:
-                minus_dc(n)
-            g0_times_o(n + 1)
+            if n > GROUPS:
+                store_dh_pair(g - 1, 0, early_dh, s_copy)
+                late_dh = dh_pair(g - 1, 1, ACC_BANKS)
             if n >= 0:
                 dz_i_and_f(n)
+            else:
+                g0_times_o(0, nc.vector, first_g0o)
             if n + 2 < STEPS:
                 tanh_a(n + 2)
                 sigmoid(n + 2, "i")
             if 0 <= n and n + 3 < STEPS:
                 load_step(n + 3)
             if half == 1:
-                store_dr_tile(0, g, dr_bank, s_copy, "out_stage")
+                for a, b in zip(dr_plan[n], dr_banks):
+                    store_dr_tile(0, a, b, s_copy, three, "out_stage")
             if 0 <= n < 3:
                 group_r(n, r_banks)
             tanh_and_square(n + 1)
             if n >= 0:
                 if_banks = transpose_dz(st[n]["dz"])
-            if n >= 1:
-                quantise_features_if(n - 1)
+            if half == 1:
+                tok_q[g, PASS_O] = quantise(keep, "tok%d_o" % g, dz_o[g], E5)
+            elif n >= 0:
+                h_q[g] = quantise(keep, "h%d" % g, grouped["h", g], E4)
             if n >= 0:
                 tok_q[g, half] = quantise(keep, "tok%d_%d" % (g, half), st[n]["dz"], E5)
             if half == 1:
-                tok_q[g, PASS_O] = quantise(keep, "tok%d_o" % g, dz_o[g], E5)
                 feat_q[g, PASS_O] = quantise(two, "feat_o", grouped["o", g], E5)
-            elif n >= 0:
-                h_q[g] = quantise(keep, "h%d" % g, grouped["h", g], E4)
             if 0 <= n < 3:
                 r_q[n] = quantise(keep, "r%d" % n, grouped["r", n], E4)
-            if n > GROUPS:
-                early_dh = dh_pair(g - 1, 0, ACC_BANKS)
             transpose_back(n + 1)
-            gate_slopes(n + 1)
             if n + 2 < STEPS:
-                sigmoid(n + 2, "f")
-            if n > GROUPS:
-                store_dh_pair(g - 1, 0, early_dh, s_copy)
-                late_dh = dh_pair(g - 1, 1, ACC_BANKS)
-            if n + 2 < STEPS:
+                gate_slopes(n + 1)
                 sigmoid(n + 2, "o")
+            else:
+                store_dh_pair(g - 1, 1, late_dh, s_copy)
             if n >= 0:
                 group_features(("if", n), "stage_if", if_banks, s_copy)
+            if n + 2 < STEPS:
+                sigmoid(n + 2, "f")
 
         n, g = STEPS - 1, GROUPS - 1
-        store_dh_pair(g - 2, 1, late_dh, s_copy)
-        psum_products(n, 0)
+        o_tiles = [dr_tile(PASS_O, a, ACC_BANKS[a], early_groups) for a in range(2)]
+        gate_slopes(n)
         quantise_features_if(n - 1)
+        store_dh_pair(g - 1, 0, dh_pair(g - 1, 0, DZT_BANKS), s_copy)
+        psum_products(n, 0)
         psum_products(n, 1)
-        early_dh = dh_pair(g - 1, 0, ACC_BANKS)
-        dr_bank = dr_tile(0, g, TC_BANKS[0])
-        store_dh_pair(g - 1, 0, early_dh, s_copy)
+        late_dh = dh_pair(g - 1, 1, (2, 3))
         o_banks = transpose_dz(dz_o[g])
-        late_dh = dh_pair(g - 1, 1, ACC_BANKS)
         minus_dc(n)
         tok_q[g, PASS_O] = quantise(keep, "tok%d_o" % g, dz_o[g], E5)
         dz_i_and_f(n)
-        store_dr_tile(0, g, dr_bank, s_copy, "i")
-        group_features(("o", g), "stage_o", o_banks, s_copy)
+        for a in range(2):
+            dr_passes(PASS_O, a, o_tiles[a], last_group)
+        o_tiles.extend([dr_tile(PASS_O, 2 + a, a, all_groups) for a in range(2)])
         store_dh_pair(g - 1, 1, late_dh, s_copy)
-        o_tiles = [dr_tile(PASS_O, a, k) for a, k in enumerate((0, 1))]
+        group_features(("o", g), "stage_o", o_banks, s_copy)
         if_banks = transpose_dz(st[n]["dz"])
-        o_tiles.extend([dr_tile(PASS_O, 2 + a, k) for a, k in enumerate((3, 2))])
         tok_q[g, 1] = quantise(keep, "tok%d_1" % g, st[n]["dz"], E5)
         feat_q[g, PASS_O] = quantise(two, "feat_o", grouped["o", g], E5)
+        for a, copy in enumerate((s_copy, v_copy)):
+            store_dr_tile(PASS_O, a, o_tiles[a], copy, four, "i")
+        if_tiles = [dr_tile(1, a, 2 + a, all_groups) for a in range(2)]
         group_features(("if", n), "stage_if", if_banks, v_copy)
-        store_dr_tile(PASS_O, 0, o_tiles[0], s_copy, "i")
-        store_dr_tile(PASS_O, 1, o_tiles[1], v_copy, "f")
+        store_dr_tile(PASS_O, 2, o_tiles[2], s_copy, four, "i")
         quantise_features_if(n)
-        store_dr_tile(PASS_O, 2, o_tiles[2], s_copy, "i")
-        store_dr_tile(PASS_O, 3, o_tiles[3], v_copy, "f")
-        for pair, banks in enumerate((ACC_BANKS, DZT_BANKS)):
-            store_dh_pair(g, pair, dh_pair(g, pair, banks), v_copy)
-        for a in range(4):
-            store_dr_tile(1, a, dr_tile(1, a, a), (s_copy, v_copy)[a % 2], ("o", "a")[a % 2])
+        store_dr_tile(PASS_O, 3, o_tiles[3], s_copy, four, "i")
+        early_dh = dh_pair(g, 0, ACC_BANKS)
+        late_dh = dh_pair(g, 1, (0, 1))
+        for a, copy in enumerate((s_copy, v_copy)):
+            store_dr_tile(1, a, if_tiles[a], copy, three, "f")
+        if_tiles = [dr_tile(1, 2 + a, DZT_BANKS[a], all_groups) for a in range(2)]
+        store_dh_pair(g, 0, early_dh, v_copy)
+        store_dh_pair(g, 1, late_dh, v_copy)
+        for a, copy in enumerate((s_copy, v_copy)):
+            store_dr_tile(1, 2 + a, if_tiles[a], copy, three, "o")

@@ -74,13 +74,16 @@ def tile_rlstmcell_pb_v_kernel(tc, inputs, h_state, c_state, c_upd, kernel, recu
         dz_o = [keep.tile([P, 2048], BF16, name="dz_o%d" % g, align_bytes=64) for g in range(GROUPS)]
         tok_q, feat_q, h_q, r_q, h_raw, r_raw, grouped = {}, {}, {}, {}, {}, {}, {}
 
-        def load_step(n):
+        sources = {"cu": (cu_hbm, 0), "i": (z_hbm, 0), "c": (c_hbm, 0), "f": (z_hbm, 1), "g0": (g0_hbm, 0),
+                   "o": (z_hbm, 2), "g1": (g1_hbm, 0)}
+
+        def load_step(n, names):
             half, g = divmod(n, GROUPS)
             cols = slice(HALF * half, HALF * (half + 1))
-            for name, src, gate in (("cu", cu_hbm, 0), ("i", z_hbm, 0), ("c", c_hbm, 0), ("f", z_hbm, 1),
-                                    ("g0", g0_hbm, 0), ("o", z_hbm, 2), ("g1", g1_hbm, 0)):
+            for name in names:
+                src, gate = sources[name]
                 dtype = F32 if src is z_hbm else BF16
-                pool = four if name == "i" else three
+                pool = four if name == "f" else three
                 t = pool.tile([P, 4, HALF], dtype, name=name, tag=name)
                 nc.sync.dma_start(out=t[:], in_=src[g][:, :, D * gate + cols.start:D * gate + cols.stop])
                 st[n][name] = t
@@ -123,10 +126,16 @@ def tile_rlstmcell_pb_v_kernel(tc, inputs, h_state, c_state, c_upd, kernel, recu
         def minus_one_times(out, gate, other):
             nc.vector.scalar_tensor_tensor(out=out, in0=gate, scalar=1.0, in1=other, op0=ALU.subtract, op1=ALU.mult)
 
-        def gate_slopes(n):
+        def slope_o(n):
+            s = st[n]
+            minus_one_times(s["o"][:], s["o"][:], s["g0o"][:])
+
+        def slope_f(n):
             s = st[n]
             minus_one_times(s["fc"][:], s["f"][:], s["fc"][:])
-            minus_one_times(s["o"][:], s["o"][:], s["g0o"][:])
+
+        def slope_i(n):
+            s = st[n]
             minus_one_times(s["a"][:], s["i"][:], s["a"][:])
 
         def new_cell_transposed(n):
@@ -172,6 +181,14 @@ def tile_rlstmcell_pb_v_kernel(tc, inputs, h_state, c_state, c_upd, kernel, recu
                             s["g0o"][:, :, cols])
             rounded_product(dz_o[g], 64 * half + 32 * q, 32, s["ntc_ps"][q][:].rearrange("p (j c) -> p j c", j=4),
                             s["o"][:, :, cols])
+
+        def last_step_tanh_and_square(n):
+            s = st[n]
+            s["ntc"] = three.tile([P, 4, HALF], F32, name="last_ntc", tag="a")
+            s["sq"] = three.tile([P, 4, HALF], F32, name="last_sq", tag="i")
+            nc.vector.tensor_tensor(out=s["ntc"][:], in0=s["a"][:], in1=s["fc"][:], op=ALU.add)
+            nc.scalar.activation(out=s["ntc"][:], in_=s["ntc"][:], func=ACT.Tanh, scale=-1.0)
+            nc.scalar.activation(out=s["sq"][:], in_=s["ntc"][:], func=ACT.Square)
 
         def minus_dc(n):
             s = st[n]
@@ -249,8 +266,8 @@ def tile_rlstmcell_pb_v_kernel(tc, inputs, h_state, c_state, c_upd, kernel, recu
             dr_passes(s, a, b, groups)
             return b
 
-        def store_dr_tile(s, a, b, copy, pool, tag):
-            stage = pool.tile([P, D], F32, name="dr_stage", tag=tag)
+        def store_dr_tile(s, a, b, copy, tag):
+            stage = three.tile([P, D], F32, name="dr_stage", tag=tag)
             copy(out=stage[:].rearrange("p (m t) -> p m t", t=4), in_=b[:].rearrange("p (t m) -> p m t", t=4))
             if s == PASS_O:
                 nc.sync.dma_start(out=dr_hbm[a][:, 2, :], in_=stage[:])
@@ -267,125 +284,156 @@ def tile_rlstmcell_pb_v_kernel(tc, inputs, h_state, c_state, c_upd, kernel, recu
 
         ctx.enter_context(tc.manual_schedule())
         nc.scalar.activation(out=warm[:], in_=ident[:, 0:8], func=ACT.Sigmoid)
-        first_g0o = four.tile([P, 4, HALF], F32, name="first_g0o", tag="i")
-        load_step(0)
-        load_step(1)
+        first_g0o = four.tile([P, 4, HALF], F32, name="first_g0o", tag="f")
+        load_step(0, ("cu", "i", "c", "f", "g0", "o"))
+        load_step(1, ("cu", "i", "c", "f"))
+        load_step(0, ("g1",))
+        load_step(1, ("g0", "o", "g1"))
+        load_step(2, ("cu", "i"))
         load_h(0)
-        load_r(0)
-        load_step(2)
+        load_step(2, ("g0", "o", "c", "f", "g1"))
         load_h(1)
-        load_r(1)
-        load_r(2)
+        for s in range(3):
+            load_r(s)
         tanh_a(0)
         for gate in ("i", "f", "o"):
             sigmoid(0, gate)
+        i_times_a(0)
+        f_times_c(0)
+        new_cell_transposed(0)
+        g0_times_o(0, nc.vector, first_g0o)
+        tanh_a(1)
+        sigmoid(1, "i")
+        slope_i(0)
+        slope_o(0)
+        i_times_a(1)
+        tanh_and_square(0)
+        sigmoid(1, "f")
+        transpose_back(0)
+        slope_f(0)
+        f_times_c(1)
+        sigmoid(1, "o")
 
         all_groups, early_groups, last_group = range(GROUPS), range(GROUPS - 1), (GROUPS - 1,)
-        dr_plan = {4: (0, 1), 5: (2,), 6: (3,)}
         late_dh = None
-        for n in range(-1, STEPS - 1):
+        for n in range(STEPS - 2):
             half, g = divmod(n, GROUPS)
-            if n >= 0:
-                g0_times_o(n + 1, nc.gpsimd, st[n]["i"])
-                psum_products(n, 0)
-                psum_products(n, 1)
-            if late_dh is not None:
-                store_dh_pair(n - 2 - GROUPS, 1, late_dh, v_copy)
-                late_dh = None
+            g0_times_o(n + 1, nc.gpsimd, st[n]["f"])
+            psum_products(n, 0)
             if half == 1:
+                dr_banks = [dr_tile(0, 2 * g + k, 2 + k, all_groups) for k in range(2)]
+            psum_products(n, 1)
+            if half == 1:
+                for k in range(2):
+                    store_dr_tile(0, 2 * g + k, dr_banks[k], s_copy, "out_stage")
                 o_banks = transpose_dz(dz_o[g])
+                group_features(("o", g), "stage_o", o_banks, s_copy)
+            elif n >= 1:
+                group_r(n - 1, transpose_r(n - 1))
+            if n >= 1:
+                i_times_a(n + 1)
+                f_times_c(n + 1)
+            new_cell_transposed(n + 1)
+            minus_dc(n)
             if n >= 1:
                 quantise_features_if(n - 1)
-            i_times_a(n + 1)
-            if n >= 0:
-                minus_dc(n)
-            f_times_c(n + 1)
             if n > GROUPS:
                 early_dh = dh_pair(g - 1, 0, ACC_BANKS)
-            if half == 1:
-                group_features(("o", g), "stage_o", o_banks, s_copy)
-                dr_banks = [dr_tile(0, a, 2 + k, all_groups) for k, a in enumerate(dr_plan[n])]
-            elif n >= 0:
+            dz_i_and_f(n)
+            tanh_a(n + 2)
+            sigmoid(n + 2, "i")
+            if n + 3 < STEPS:
+                load_step(n + 3, sources)
+            if half == 0:
                 group_h(g)
                 if g + 2 < GROUPS:
                     load_h(g + 2)
-            if 0 <= n < 3:
-                r_banks = transpose_r(n)
-            new_cell_transposed(n + 1)
+            tanh_and_square(n + 1)
+            if half == 1:
+                tok_q[g, PASS_O] = quantise(keep, "tok%d_o" % g, dz_o[g], E5)
+            elif n >= 1:
+                r_q[n - 1] = quantise(keep, "r%d" % (n - 1), grouped["r", n - 1], E4)
+            tok_q[g, half] = quantise(keep, "tok%d_%d" % (g, half), st[n]["dz"], E5)
+            if half == 1:
+                feat_q[g, PASS_O] = quantise(two, "feat_o", grouped["o", g], E5)
+            else:
+                h_q[g] = quantise(keep, "h%d" % g, grouped["h", g], E4)
+            transpose_back(n + 1)
+            if_banks = transpose_dz(st[n]["dz"])
             if n > GROUPS:
                 store_dh_pair(g - 1, 0, early_dh, s_copy)
                 late_dh = dh_pair(g - 1, 1, ACC_BANKS)
-            if n >= 0:
-                dz_i_and_f(n)
-            else:
-                g0_times_o(0, nc.vector, first_g0o)
-            if n + 2 < STEPS:
-                tanh_a(n + 2)
-                sigmoid(n + 2, "i")
-            if 0 <= n and n + 3 < STEPS:
-                load_step(n + 3)
-            if half == 1:
-                for a, b in zip(dr_plan[n], dr_banks):
-                    store_dr_tile(0, a, b, s_copy, three, "out_stage")
-            if 0 <= n < 3:
-                group_r(n, r_banks)
-            tanh_and_square(n + 1)
-            if n >= 0:
-                if_banks = transpose_dz(st[n]["dz"])
-            if half == 1:
-                tok_q[g, PASS_O] = quantise(keep, "tok%d_o" % g, dz_o[g], E5)
-            elif n >= 0:
-                h_q[g] = quantise(keep, "h%d" % g, grouped["h", g], E4)
-            if n >= 0:
-                tok_q[g, half] = quantise(keep, "tok%d_%d" % (g, half), st[n]["dz"], E5)
-            if half == 1:
-                feat_q[g, PASS_O] = quantise(two, "feat_o", grouped["o", g], E5)
-            if 0 <= n < 3:
-                r_q[n] = quantise(keep, "r%d" % n, grouped["r", n], E4)
-            transpose_back(n + 1)
-            if n + 2 < STEPS:
-                gate_slopes(n + 1)
-                sigmoid(n + 2, "o")
-            else:
-                store_dh_pair(g - 1, 1, late_dh, s_copy)
-            if n >= 0:
-                group_features(("if", n), "stage_if", if_banks, s_copy)
-            if n + 2 < STEPS:
-                sigmoid(n + 2, "f")
+            slope_o(n + 1)
+            slope_f(n + 1)
+            slope_i(n + 1)
+            sigmoid(n + 2, "o")
+            group_features(("if", n), "stage_if", if_banks, s_copy)
+            sigmoid(n + 2, "f")
 
-        n, g = STEPS - 1, GROUPS - 1
-        o_tiles = [dr_tile(PASS_O, a, ACC_BANKS[a], early_groups) for a in range(2)]
-        gate_slopes(n)
-        quantise_features_if(n - 1)
-        store_dh_pair(g - 1, 0, dh_pair(g - 1, 0, DZT_BANKS), s_copy)
+        n, g = STEPS - 2, GROUPS - 2
+        g0_times_o(n + 1, nc.gpsimd, st[n]["f"])
         psum_products(n, 0)
         psum_products(n, 1)
-        late_dh = dh_pair(g - 1, 1, (2, 3))
+        store_dh_pair(g - 2, 1, late_dh, s_copy)
         o_banks = transpose_dz(dz_o[g])
+        group_features(("o", g), "stage_o", o_banks, s_copy)
+        i_times_a(n + 1)
+        quantise_features_if(n - 1)
+        early_dh = dh_pair(g - 1, 0, ACC_BANKS)
+        late_dh = dh_pair(g - 1, 1, (2, 3))
+        f_times_c(n + 1)
         minus_dc(n)
         tok_q[g, PASS_O] = quantise(keep, "tok%d_o" % g, dz_o[g], E5)
         dz_i_and_f(n)
-        for a in range(2):
-            dr_passes(PASS_O, a, o_tiles[a], last_group)
-        o_tiles.extend([dr_tile(PASS_O, 2 + a, a, all_groups) for a in range(2)])
+        store_dh_pair(g - 1, 0, early_dh, s_copy)
         store_dh_pair(g - 1, 1, late_dh, s_copy)
-        group_features(("o", g), "stage_o", o_banks, s_copy)
+        o_tiles = [dr_tile(PASS_O, a, a, early_groups) for a in range(4)]
         if_banks = transpose_dz(st[n]["dz"])
+        last_step_tanh_and_square(n + 1)
         tok_q[g, 1] = quantise(keep, "tok%d_1" % g, st[n]["dz"], E5)
         feat_q[g, PASS_O] = quantise(two, "feat_o", grouped["o", g], E5)
-        for a, copy in enumerate((s_copy, v_copy)):
-            store_dr_tile(PASS_O, a, o_tiles[a], copy, four, "i")
-        if_tiles = [dr_tile(1, a, 2 + a, all_groups) for a in range(2)]
+        if_tiles = [dr_tile(1, a, ACC_BANKS[a], early_groups) for a in range(2)]
+        group_features(("if", n), "stage_if", if_banks, s_copy)
+
+        n, g = STEPS - 1, GROUPS - 1
+        s = st[n]
+        slope_o(n)
+        slope_i(n)
+        rounded_product(dz_o[g], 64, 64, s["ntc"][:], s["o"][:])
+        quantise_features_if(n - 1)
+        tok_q[g, PASS_O] = quantise(keep, "tok%d_o" % g, dz_o[g], E5)
+        early_dh = dh_pair(g - 1, 0, DZT_BANKS)
+        for a in range(4):
+            dr_passes(PASS_O, a, o_tiles[a], last_group)
+        store_dh_pair(g - 1, 0, early_dh, s_copy)
+        o_banks = transpose_dz(dz_o[g])
+        for a in range(2):
+            store_dr_tile(PASS_O, a, o_tiles[a], s_copy, "cu")
+        late_dh = dh_pair(g - 1, 1, (0, 1))
+        for a in range(2, 4):
+            store_dr_tile(PASS_O, a, o_tiles[a], s_copy, "c")
+        group_features(("o", g), "stage_o", o_banks, s_copy)
+        if_tiles.extend([dr_tile(1, 2 + a, 2 + a, early_groups) for a in range(2)])
+        minus_one_times(s["g0o"][:], s["sq"][:], s["g0o"][:])
+        slope_f(n)
+        minus_dc(n)
+        dz_i_and_f(n)
+        feat_q[g, PASS_O] = quantise(two, "feat_o", grouped["o", g], E5)
+        store_dh_pair(g - 1, 1, late_dh, s_copy)
+        if_banks = transpose_dz(st[n]["dz"])
+        tok_q[g, 1] = quantise(keep, "tok%d_1" % g, st[n]["dz"], E5)
+        for a in range(4):
+            dr_passes(1, a, if_tiles[a], last_group)
         group_features(("if", n), "stage_if", if_banks, v_copy)
-        store_dr_tile(PASS_O, 2, o_tiles[2], s_copy, four, "i")
         quantise_features_if(n)
-        store_dr_tile(PASS_O, 3, o_tiles[3], s_copy, four, "i")
-        early_dh = dh_pair(g, 0, ACC_BANKS)
-        late_dh = dh_pair(g, 1, (0, 1))
-        for a, copy in enumerate((s_copy, v_copy)):
-            store_dr_tile(1, a, if_tiles[a], copy, three, "f")
-        if_tiles = [dr_tile(1, 2 + a, DZT_BANKS[a], all_groups) for a in range(2)]
-        store_dh_pair(g, 0, early_dh, v_copy)
-        store_dh_pair(g, 1, late_dh, v_copy)
-        for a, copy in enumerate((s_copy, v_copy)):
-            store_dr_tile(1, 2 + a, if_tiles[a], copy, three, "o")
+        dh_banks = [bank(k) for k in (0, 1) + DZT_BANKS]
+        for pair in range(2):
+            for passes in ((0, PASS_O), (1,)):
+                for j in (2 * pair, 2 * pair + 1):
+                    dh_passes(g, j, dh_banks[j], passes)
+        for a, copy in enumerate((s_copy, s_copy, v_copy, s_copy)):
+            store_dr_tile(1, a, if_tiles[a], copy, ("g0", "g1")[a % 2])
+        for j, copy in enumerate((v_copy, s_copy, v_copy, s_copy)):
+            stage = three.tile([P, D], F32, name="last_stage", tag=("cu", "c")[j % 2])
+            copy(out=stage[:], in_=dh_banks[j][:])
+            nc.sync.dma_start(out=dh_hbm[g][:, j, :], in_=stage[:])

@@ -21,11 +21,12 @@ GROUPS = 4
 HALF = 256
 STEPS = 8
 PASS_O = 2
-CN_BANKS = (0, 1)
-TC_BANKS = (2, 0)
-SQ_BANKS = (3, 1)
+CELL_BANKS = (0, 1)
+GRAD_BANKS = (2, 3)
 DZT_BANKS = (4, 5)
 ACC_BANKS = (6, 7)
+G1_BANK = 6
+GPSIMD_ROWS = 2
 
 
 def tile_rlstmcell_pb_v_kernel(tc, inputs, h_state, c_state, c_upd, kernel, recurrent_kernel, bias,
@@ -46,10 +47,13 @@ def tile_rlstmcell_pb_v_kernel(tc, inputs, h_state, c_state, c_upd, kernel, recu
         two = ctx.enter_context(tc.tile_pool(name="two", bufs=2))
         three = ctx.enter_context(tc.tile_pool(name="three", bufs=3))
         four = ctx.enter_context(tc.tile_pool(name="four", bufs=4))
+        six = ctx.enter_context(tc.tile_pool(name="six", bufs=6))
         psum = ctx.enter_context(tc.psum_pool(name="psum", bufs=1))
 
         ident = keep.tile([P, P], F32, name="ident")
         make_identity(nc, ident[:])
+        ident_bf = keep.tile([P, P], BF16, name="ident_bf")
+        make_identity(nc, ident_bf[:])
         warm = keep.tile([P, 8], F32, name="warm")
 
         def bank(k):
@@ -109,19 +113,26 @@ def tile_rlstmcell_pb_v_kernel(tc, inputs, h_state, c_state, c_upd, kernel, recu
         def sigmoid(n, gate):
             nc.scalar.activation(out=st[n][gate][:], in_=st[n][gate][:], func=ACT.Sigmoid)
 
-        def i_times_a(n):
+        def i_times_a(n, engine):
             s = st[n]
-            nc.vector.tensor_tensor(out=s["a"][:], in0=s["i"][:], in1=s["a"][:], op=ALU.mult)
+            engine.tensor_tensor(out=s["a"][:], in0=s["i"][:], in1=s["a"][:], op=ALU.mult)
 
-        def f_times_c(n):
+        def f_times_c(n, engine, out):
             s = st[n]
-            s["fc"] = two.tile([P, 4, HALF], F32, name="fc", tag="fc")
-            nc.vector.tensor_tensor(out=s["fc"][:], in0=s["f"][:], in1=s["c"][:], op=ALU.mult)
+            s["fc"] = out
+            engine.tensor_tensor(out=out[:], in0=s["f"][:], in1=s["c"][:], op=ALU.mult)
 
-        def g0_times_o(n, engine, out):
+        def g0_times_o(n, engine, rows):
             s = st[n]
-            s["g0o"] = out
-            engine.tensor_tensor(out=out[:], in0=s["o"][:], in1=s["g0"][:], op=ALU.mult)
+            if "g0o" not in s:
+                s["g0o"] = two.tile([P, 4, HALF], F32, name="g0o", tag="g0o")
+            engine.tensor_tensor(out=s["g0o"][:, rows], in0=s["o"][:, rows], in1=s["g0"][:, rows], op=ALU.mult)
+
+        def gpsimd_products(n):
+            f_times_c(n + 1, nc.gpsimd, st[n]["f"])
+            if n >= 1:
+                i_times_a(n + 1, nc.gpsimd)
+            g0_times_o(n + 1, nc.gpsimd, slice(0, GPSIMD_ROWS if n >= 1 else 4))
 
         def minus_one_times(out, gate, other):
             nc.vector.scalar_tensor_tensor(out=out, in0=gate, scalar=1.0, in1=other, op0=ALU.subtract, op1=ALU.mult)
@@ -142,7 +153,7 @@ def tile_rlstmcell_pb_v_kernel(tc, inputs, h_state, c_state, c_upd, kernel, recu
             s = st[n]
             s["cn"] = []
             for q in range(2):
-                b = bank(CN_BANKS[q])
+                b = bank(CELL_BANKS[q])
                 for j in range(4):
                     for k, term in enumerate(("a", "fc")):
                         nc.tensor.matmul(out=b[:, P * j:P * (j + 1)], lhsT=s[term][:, j, P * q:P * (q + 1)],
@@ -158,37 +169,59 @@ def tile_rlstmcell_pb_v_kernel(tc, inputs, h_state, c_state, c_upd, kernel, recu
             for q in range(2):
                 nc.scalar.activation(out=s["sq"][q][:], in_=s["ntc"][q][:], func=ACT.Square)
 
-        def transpose_back(n):
+        def transpose_back(src, k):
+            b = bank(k)
+            for j in range(4):
+                nc.tensor.transpose(b[:, P * j:P * (j + 1)], src[:, P * j:P * (j + 1)], ident[:])
+            return b[:].rearrange("p (j c) -> p j c", j=4)
+
+        def tanh_back(n):
+            st[n]["ntc_ps"] = [transpose_back(st[n]["ntc"][q], CELL_BANKS[q]) for q in range(2)]
+
+        def g0o_transposed(n):
             s = st[n]
-            for name, banks in (("ntc", TC_BANKS), ("sq", SQ_BANKS)):
-                s[name + "_ps"] = []
-                for q in range(2):
-                    b = bank(banks[q])
-                    for j in range(4):
-                        nc.tensor.transpose(b[:, P * j:P * (j + 1)], s[name][q][:, P * j:P * (j + 1)], ident[:])
-                    s[name + "_ps"].append(b)
+            s["g0o_ps"] = []
+            for q in range(2):
+                b = bank(GRAD_BANKS[q])
+                for j in range(4):
+                    nc.tensor.transpose(b[:, P * j:P * (j + 1)], s["g0o"][:, j, P * q:P * (q + 1)], ident[:])
+                s["g0o_ps"].append(b)
+
+        def g1_transposed(n):
+            s = st[n]
+            s["g1_ps"] = psum.tile([P, 2, 512], BF16, name="g1_bank", tag="bank%d" % G1_BANK)
+            for q in range(2):
+                for j in range(4):
+                    nc.tensor.transpose(s["g1_ps"][:, q, P * j:P * (j + 1)], s["g1"][:, j, P * q:P * (q + 1)],
+                                        ident_bf[:])
 
         def rounded_product(dz, first, count, in0, in1):
             out = dz[:].rearrange("p (t m j) -> p m j t", t=4, j=4)[:, first:first + count]
             nc.vector.tensor_tensor(out=out, in0=in0.rearrange("p j (m t) -> p m j t", t=4),
                                     in1=in1.rearrange("p j (m t) -> p m j t", t=4), op=ALU.mult)
 
-        def psum_products(n, q):
+        def psum_products(n):
             half, g = divmod(n, GROUPS)
             s = st[n]
-            cols = slice(P * q, P * (q + 1))
-            minus_one_times(s["g0o"][:, :, cols], s["sq_ps"][q][:].rearrange("p (j c) -> p j c", j=4),
-                            s["g0o"][:, :, cols])
-            rounded_product(dz_o[g], 64 * half + 32 * q, 32, s["ntc_ps"][q][:].rearrange("p (j c) -> p j c", j=4),
-                            s["o"][:, :, cols])
+            for q in range(2):
+                minus_one_times(s["sq"][q][:], s["sq"][q][:], s["g0o_ps"][q][:])
+            for q in range(2):
+                nc.vector.tensor_tensor(out=s["sq"][q][:], in0=s["sq"][q][:], in1=s["g1_ps"][:, q, :],
+                                        op=ALU.subtract)
+            ndc_ps = [transpose_back(s["sq"][q], GRAD_BANKS[q]) for q in range(2)]
+            for q in range(2):
+                rounded_product(dz_o[g], 64 * half + 32 * q, 32, s["ntc_ps"][q], s["o"][:, :, P * q:P * (q + 1)])
+            s["dz"] = two.tile([P, 2048], BF16, name="dz_if", tag="dz_if", align_bytes=64)
+            for q in range(2):
+                for gate, slope in enumerate(("a", "fc")):
+                    rounded_product(s["dz"], 64 * gate + 32 * q, 32, ndc_ps[q], s[slope][:, :, P * q:P * (q + 1)])
 
-        def last_step_tanh_and_square(n):
+        def last_step_tanh(n):
             s = st[n]
             s["ntc"] = three.tile([P, 4, HALF], F32, name="last_ntc", tag="a")
             s["sq"] = three.tile([P, 4, HALF], F32, name="last_sq", tag="i")
             nc.vector.tensor_tensor(out=s["ntc"][:], in0=s["a"][:], in1=s["fc"][:], op=ALU.add)
             nc.scalar.activation(out=s["ntc"][:], in_=s["ntc"][:], func=ACT.Tanh, scale=-1.0)
-            nc.scalar.activation(out=s["sq"][:], in_=s["ntc"][:], func=ACT.Square)
 
         def minus_dc(n):
             s = st[n]
@@ -225,7 +258,7 @@ def tile_rlstmcell_pb_v_kernel(tc, inputs, h_state, c_state, c_upd, kernel, recu
             words = r_raw[s][:].rearrange("p a k -> p (a k)").bitcast(F32)
             banks = []
             for pair in range(2):
-                b = bank(ACC_BANKS[pair])
+                b = bank(DZT_BANKS[pair])
                 for a in range(2):
                     for u in range(2):
                         first = 256 * (2 * pair + a)
@@ -251,11 +284,9 @@ def tile_rlstmcell_pb_v_kernel(tc, inputs, h_state, c_state, c_upd, kernel, recu
                 dh_passes(g, 2 * pair + e, banks[e], (0, PASS_O, 1))
             return banks
 
-        def store_dh_pair(g, pair, banks, second_engine_copy):
-            stage = three.tile([P, 2, D], F32, name="dh_stage", tag="out_stage")
-            for e, copy in enumerate((nc.scalar.copy, second_engine_copy)):
-                copy(out=stage[:, e, :], in_=banks[e][:])
-            nc.sync.dma_start(out=dh_hbm[g][:, 2 * pair:2 * pair + 2, :], in_=stage[:])
+        def store_dh_pair(g, pair, banks):
+            for e in range(2):
+                store_dh_tile(g, 2 * pair + e, banks[e], nc.scalar.copy)
 
         def dr_passes(s, a, b, groups):
             for g in groups:
@@ -266,14 +297,32 @@ def tile_rlstmcell_pb_v_kernel(tc, inputs, h_state, c_state, c_upd, kernel, recu
             dr_passes(s, a, b, groups)
             return b
 
-        def store_dr_tile(s, a, b, copy, tag):
-            stage = three.tile([P, D], F32, name="dr_stage", tag=tag)
+        def store_dr_tile(s, a, b, copy):
+            stage = six.tile([P, D], F32, name="dr_stage", tag="out_tile")
             copy(out=stage[:].rearrange("p (m t) -> p m t", t=4), in_=b[:].rearrange("p (t m) -> p m t", t=4))
             if s == PASS_O:
                 nc.sync.dma_start(out=dr_hbm[a][:, 2, :], in_=stage[:])
             else:
                 nc.sync.dma_start(out=dr_hbm[a][:, 0:2, HALF * s:HALF * (s + 1)],
                                   in_=stage[:].rearrange("p (gate c) -> p gate c", gate=2))
+
+        def store_dh_tile(g, j, b, copy):
+            stage = six.tile([P, D], F32, name="dh_stage", tag="out_tile")
+            copy(out=stage[:], in_=b[:])
+            nc.sync.dma_start(out=dh_hbm[g][:, j, :], in_=stage[:])
+
+        def output_tile(g, k, bank_number):
+            if g == 0:
+                return dr_tile(0, k, bank_number, range(GROUPS))
+            b = bank(bank_number)
+            dh_passes(g - 1, k, b, (0, PASS_O, 1))
+            return b
+
+        def store_output(g, k, b, copy):
+            if g == 0:
+                store_dr_tile(0, k, b, copy)
+            else:
+                store_dh_tile(g - 1, k, b, copy)
 
         def quantise_features_if(n):
             half, g = divmod(n, GROUPS)
@@ -284,156 +333,154 @@ def tile_rlstmcell_pb_v_kernel(tc, inputs, h_state, c_state, c_upd, kernel, recu
 
         ctx.enter_context(tc.manual_schedule())
         nc.scalar.activation(out=warm[:], in_=ident[:, 0:8], func=ACT.Sigmoid)
-        first_g0o = four.tile([P, 4, HALF], F32, name="first_g0o", tag="f")
-        load_step(0, ("cu", "i", "c", "f", "g0", "o"))
-        load_step(1, ("cu", "i", "c", "f"))
-        load_step(0, ("g1",))
-        load_step(1, ("g0", "o", "g1"))
+        first_fc = four.tile([P, 4, HALF], F32, name="first_fc", tag="f")
+        load_step(0, ("cu", "i", "c", "f", "g0", "o", "g1"))
+        load_step(1, ("cu", "i", "c", "f", "g0", "o", "g1"))
         load_step(2, ("cu", "i"))
         load_h(0)
-        load_step(2, ("g0", "o", "c", "f", "g1"))
+        load_step(2, ("c", "f", "g0", "o", "g1"))
         load_h(1)
-        for s in range(3):
-            load_r(s)
         tanh_a(0)
         for gate in ("i", "f", "o"):
             sigmoid(0, gate)
-        i_times_a(0)
-        f_times_c(0)
+        i_times_a(0, nc.vector)
+        f_times_c(0, nc.vector, first_fc)
         new_cell_transposed(0)
-        g0_times_o(0, nc.vector, first_g0o)
+        g0_times_o(0, nc.vector, slice(0, 4))
+        g0o_transposed(0)
+        g1_transposed(0)
         tanh_a(1)
+        tanh_and_square(0)
+        tanh_back(0)
         sigmoid(1, "i")
+        sigmoid(1, "f")
         slope_i(0)
         slope_o(0)
-        i_times_a(1)
-        tanh_and_square(0)
-        sigmoid(1, "f")
-        transpose_back(0)
         slope_f(0)
-        f_times_c(1)
-        sigmoid(1, "o")
+        i_times_a(1, nc.vector)
 
         all_groups, early_groups, last_group = range(GROUPS), range(GROUPS - 1), (GROUPS - 1,)
-        late_dh = None
+        outputs = {}
         for n in range(STEPS - 2):
             half, g = divmod(n, GROUPS)
-            g0_times_o(n + 1, nc.gpsimd, st[n]["f"])
-            psum_products(n, 0)
-            if half == 1:
-                dr_banks = [dr_tile(0, 2 * g + k, 2 + k, all_groups) for k in range(2)]
-            psum_products(n, 1)
-            if half == 1:
-                for k in range(2):
-                    store_dr_tile(0, 2 * g + k, dr_banks[k], s_copy, "out_stage")
-                o_banks = transpose_dz(dz_o[g])
-                group_features(("o", g), "stage_o", o_banks, s_copy)
-            elif n >= 1:
-                group_r(n - 1, transpose_r(n - 1))
-            if n >= 1:
-                i_times_a(n + 1)
-                f_times_c(n + 1)
-            new_cell_transposed(n + 1)
-            minus_dc(n)
-            if n >= 1:
-                quantise_features_if(n - 1)
+            with_r = 2 <= n < 5
+            sigmoid(n + 1, "o")
+            gpsimd_products(n)
+            if with_r:
+                group_r(n - 2, transpose_r(n - 2))
             if n > GROUPS:
-                early_dh = dh_pair(g - 1, 0, ACC_BANKS)
-            dz_i_and_f(n)
-            tanh_a(n + 2)
-            sigmoid(n + 2, "i")
-            if n + 3 < STEPS:
-                load_step(n + 3, sources)
-            if half == 0:
+                outputs[3] = output_tile(g - 1, 3, ACC_BANKS[1])
+            psum_products(n)
+            if half == 1:
+                o_banks = transpose_dz(dz_o[g])
+                if g >= 1:
+                    outputs[2] = output_tile(g - 1, 2, ACC_BANKS[0])
+                    store_output(g - 1, 3, outputs[3], v_copy)
+            else:
                 group_h(g)
                 if g + 2 < GROUPS:
                     load_h(g + 2)
-            tanh_and_square(n + 1)
+            tanh_a(n + 2)
+            sigmoid(n + 2, "i")
             if half == 1:
-                tok_q[g, PASS_O] = quantise(keep, "tok%d_o" % g, dz_o[g], E5)
-            elif n >= 1:
-                r_q[n - 1] = quantise(keep, "r%d" % (n - 1), grouped["r", n - 1], E4)
+                group_features(("o", g), "stage_o", o_banks, s_copy)
+            if n > GROUPS:
+                store_output(g - 1, 2, outputs[2], s_copy)
+            new_cell_transposed(n + 1)
+            if n + 3 < STEPS:
+                load_step(n + 3, sources)
+            if n < 3:
+                load_r(n)
+            if 1 <= n:
+                quantise_features_if(n - 1)
+                g0_times_o(n + 1, nc.vector, slice(GPSIMD_ROWS, 4))
+            if half == 1:
+                for k in range(2):
+                    outputs[k] = output_tile(g, k, GRAD_BANKS[k])
+            if_banks = transpose_dz(st[n]["dz"])
+            tanh_and_square(n + 1)
+            if with_r:
+                r_q[n - 2] = quantise(keep, "r%d" % (n - 2), grouped["r", n - 2], E4)
             tok_q[g, half] = quantise(keep, "tok%d_%d" % (g, half), st[n]["dz"], E5)
             if half == 1:
+                tok_q[g, PASS_O] = quantise(keep, "tok%d_o" % g, dz_o[g], E5)
                 feat_q[g, PASS_O] = quantise(two, "feat_o", grouped["o", g], E5)
+                for k in range(2):
+                    store_output(g, k, outputs[k], s_copy)
             else:
                 h_q[g] = quantise(keep, "h%d" % g, grouped["h", g], E4)
-            transpose_back(n + 1)
-            if_banks = transpose_dz(st[n]["dz"])
-            if n > GROUPS:
-                store_dh_pair(g - 1, 0, early_dh, s_copy)
-                late_dh = dh_pair(g - 1, 1, ACC_BANKS)
+            g0o_transposed(n + 1)
+            tanh_back(n + 1)
+            g1_transposed(n + 1)
             slope_o(n + 1)
             slope_f(n + 1)
             slope_i(n + 1)
-            sigmoid(n + 2, "o")
-            group_features(("if", n), "stage_if", if_banks, s_copy)
             sigmoid(n + 2, "f")
+            group_features(("if", n), "stage_if", if_banks, s_copy)
 
         n, g = STEPS - 2, GROUPS - 2
-        g0_times_o(n + 1, nc.gpsimd, st[n]["f"])
-        psum_products(n, 0)
-        psum_products(n, 1)
-        store_dh_pair(g - 2, 1, late_dh, s_copy)
+        s = st[n + 1]
+        sigmoid(n + 1, "o")
+        gpsimd_products(n)
+        outputs[3] = output_tile(g - 1, 3, ACC_BANKS[1])
+        psum_products(n)
         o_banks = transpose_dz(dz_o[g])
+        outputs[2] = output_tile(g - 1, 2, ACC_BANKS[0])
+        store_output(g - 1, 3, outputs[3], v_copy)
         group_features(("o", g), "stage_o", o_banks, s_copy)
-        i_times_a(n + 1)
+        store_output(g - 1, 2, outputs[2], s_copy)
         quantise_features_if(n - 1)
-        early_dh = dh_pair(g - 1, 0, ACC_BANKS)
-        late_dh = dh_pair(g - 1, 1, (2, 3))
-        f_times_c(n + 1)
-        minus_dc(n)
-        tok_q[g, PASS_O] = quantise(keep, "tok%d_o" % g, dz_o[g], E5)
-        dz_i_and_f(n)
-        store_dh_pair(g - 1, 0, early_dh, s_copy)
-        store_dh_pair(g - 1, 1, late_dh, s_copy)
-        o_tiles = [dr_tile(PASS_O, a, a, early_groups) for a in range(4)]
+        early_dh = dh_pair(g - 1, 0, CELL_BANKS)
         if_banks = transpose_dz(st[n]["dz"])
-        last_step_tanh_and_square(n + 1)
+        late_dh = dh_pair(g - 1, 1, GRAD_BANKS)
+        last_step_tanh(n + 1)
         tok_q[g, 1] = quantise(keep, "tok%d_1" % g, st[n]["dz"], E5)
+        tok_q[g, PASS_O] = quantise(keep, "tok%d_o" % g, dz_o[g], E5)
+        g0_times_o(n + 1, nc.vector, slice(GPSIMD_ROWS, 4))
         feat_q[g, PASS_O] = quantise(two, "feat_o", grouped["o", g], E5)
-        if_tiles = [dr_tile(1, a, ACC_BANKS[a], early_groups) for a in range(2)]
+        store_dh_pair(g - 1, 0, early_dh)
         group_features(("if", n), "stage_if", if_banks, s_copy)
+        nc.scalar.activation(out=s["sq"][:], in_=s["ntc"][:], func=ACT.Square)
+        store_dh_pair(g - 1, 1, late_dh)
+        if_tiles = [dr_tile(1, a, ACC_BANKS[a], early_groups) for a in range(2)]
+        o_tiles = [dr_tile(PASS_O, a, a, early_groups) for a in range(2)]
 
         n, g = STEPS - 1, GROUPS - 1
-        s = st[n]
         slope_o(n)
         slope_i(n)
-        rounded_product(dz_o[g], 64, 64, s["ntc"][:], s["o"][:])
         quantise_features_if(n - 1)
-        tok_q[g, PASS_O] = quantise(keep, "tok%d_o" % g, dz_o[g], E5)
         early_dh = dh_pair(g - 1, 0, DZT_BANKS)
+        o_tiles.extend([dr_tile(PASS_O, a, a, early_groups) for a in range(2, 4)])
+        rounded_product(dz_o[g], 64, 64, s["ntc"][:], s["o"][:])
+        minus_one_times(s["g0o"][:], s["sq"][:], s["g0o"][:])
+        tok_q[g, PASS_O] = quantise(keep, "tok%d_o" % g, dz_o[g], E5)
         for a in range(4):
             dr_passes(PASS_O, a, o_tiles[a], last_group)
-        store_dh_pair(g - 1, 0, early_dh, s_copy)
+        store_dh_pair(g - 1, 0, early_dh)
         o_banks = transpose_dz(dz_o[g])
-        for a in range(2):
-            store_dr_tile(PASS_O, a, o_tiles[a], s_copy, "cu")
-        late_dh = dh_pair(g - 1, 1, (0, 1))
-        for a in range(2, 4):
-            store_dr_tile(PASS_O, a, o_tiles[a], s_copy, "c")
+        for a in range(4):
+            store_dr_tile(PASS_O, a, o_tiles[a], s_copy)
+        late_dh = dh_pair(g - 1, 1, CELL_BANKS)
+        if_tiles.extend([dr_tile(1, 2 + a, GRAD_BANKS[a], early_groups) for a in range(2)])
         group_features(("o", g), "stage_o", o_banks, s_copy)
-        if_tiles.extend([dr_tile(1, 2 + a, 2 + a, early_groups) for a in range(2)])
-        minus_one_times(s["g0o"][:], s["sq"][:], s["g0o"][:])
-        slope_f(n)
         minus_dc(n)
+        slope_f(n)
         dz_i_and_f(n)
+        if_banks = transpose_dz(s["dz"])
+        store_dh_tile(g - 1, 2, late_dh[0], v_copy)
+        tok_q[g, 1] = quantise(keep, "tok%d_1" % g, s["dz"], E5)
+        store_dh_tile(g - 1, 3, late_dh[1], s_copy)
         feat_q[g, PASS_O] = quantise(two, "feat_o", grouped["o", g], E5)
-        store_dh_pair(g - 1, 1, late_dh, s_copy)
-        if_banks = transpose_dz(st[n]["dz"])
-        tok_q[g, 1] = quantise(keep, "tok%d_1" % g, st[n]["dz"], E5)
         for a in range(4):
             dr_passes(1, a, if_tiles[a], last_group)
         group_features(("if", n), "stage_if", if_banks, v_copy)
         quantise_features_if(n)
-        dh_banks = [bank(k) for k in (0, 1) + DZT_BANKS]
+        dh_banks = [bank(k) for k in CELL_BANKS + DZT_BANKS]
         for pair in range(2):
             for passes in ((0, PASS_O), (1,)):
                 for j in (2 * pair, 2 * pair + 1):
                     dh_passes(g, j, dh_banks[j], passes)
         for a, copy in enumerate((s_copy, s_copy, v_copy, s_copy)):
-            store_dr_tile(1, a, if_tiles[a], copy, ("g0", "g1")[a % 2])
+            store_dr_tile(1, a, if_tiles[a], copy)
         for j, copy in enumerate((v_copy, s_copy, v_copy, s_copy)):
-            stage = three.tile([P, D], F32, name="last_stage", tag=("cu", "c")[j % 2])
-            copy(out=stage[:], in_=dh_banks[j][:])
-            nc.sync.dma_start(out=dh_hbm[g][:, j, :], in_=stage[:])
+            store_dh_tile(g, j, dh_banks[j], copy)

@@ -17,14 +17,17 @@ ACT = mybir.ActivationFunctionType
 ALU = mybir.AluOpType
 
 P = 128
-GROUPS = 4
-HALF = 256
-STEPS = 8
+GROUPS = T // 512
+HALF = D // 2
 PASS_O = 2
+STEP_ORDER = ((0, 0), (0, 1), (1, 0), (1, 1), (2, 0), (3, 0), (2, 1), (3, 1))
+STEPS = len(STEP_ORDER)
+FIRST_OUTPUT_STEP = 3
+FIRST_HALVES_DONE = 5
 CELL_BANKS = (0, 1)
 GRAD_BANKS = (2, 3)
 DZT_BANKS = (4, 5)
-ACC_BANKS = (6, 7)
+SPARE_BANKS = (6, 7)
 G1_BANK = 6
 GPSIMD_ROWS = 2
 
@@ -47,191 +50,176 @@ def tile_rlstmcell_pb_v_kernel(tc, inputs, h_state, c_state, c_upd, kernel, recu
         two = ctx.enter_context(tc.tile_pool(name="two", bufs=2))
         three = ctx.enter_context(tc.tile_pool(name="three", bufs=3))
         four = ctx.enter_context(tc.tile_pool(name="four", bufs=4))
-        six = ctx.enter_context(tc.tile_pool(name="six", bufs=6))
+        eight = ctx.enter_context(tc.tile_pool(name="eight", bufs=8))
         psum = ctx.enter_context(tc.psum_pool(name="psum", bufs=1))
 
         ident = keep.tile([P, P], F32, name="ident")
         make_identity(nc, ident[:])
         ident_bf = keep.tile([P, P], BF16, name="ident_bf")
         make_identity(nc, ident_bf[:])
-        warm = keep.tile([P, 8], F32, name="warm")
 
-        def bank(k):
-            return psum.tile([P, 512], F32, name="bank%d" % k, tag="bank%d" % k)
-
-        def quantised(pool, name):
-            codes = pool.tile([P, 512], U32, name=name + "_codes", tag=name + "_codes", align_bytes=64)
-            scales = pool.tile([P, 512], U8, name=name + "_scales", tag=name + "_scales", align_bytes=64)
-            return codes, scales
+        def bank(number):
+            return psum.tile([P, 512], F32, name="bank%d" % number, tag="bank%d" % number)
 
         def quantise(pool, name, src, fmt):
-            codes, scales = quantised(pool, name)
+            codes = pool.tile([P, 512], U32, name=name + "_codes", tag=name + "_codes", align_bytes=64)
+            scales = pool.tile([P, 512], U8, name=name + "_scales", tag=name + "_scales", align_bytes=64)
             nc.vector.quantize_mx(out=codes[:].bitcast(fmt), scales=scales[:], in_=src[:])
             return codes, scales
 
-        def mx(out, lhs, lhs_fmt, col, rhs, rhs_fmt, start, stop):
-            cols = slice(P * col, P * (col + 1))
+        def mx(out, lhs, lhs_fmt, lhs_tile, rhs, rhs_fmt, start, stop):
+            cols = slice(P * lhs_tile, P * (lhs_tile + 1))
             nc.tensor.matmul_mx(out=out[:], lhsT=lhs[0][:, cols].bitcast(lhs_fmt), lhsT_scale=lhs[1][:, cols],
                                 rhs=rhs[0][:].bitcast(rhs_fmt), rhs_scale=rhs[1][:], start=start, stop=stop)
 
-        st = [dict() for n in range(STEPS)]
-        dz_o = [keep.tile([P, 2048], BF16, name="dz_o%d" % g, align_bytes=64) for g in range(GROUPS)]
-        tok_q, feat_q, h_q, r_q, h_raw, r_raw, grouped = {}, {}, {}, {}, {}, {}, {}
+        steps = [dict() for n in range(STEPS)]
+        dz_o = {}
+        tok_q, feat_q = {}, {}
+        h_q, r_q, h_raw, r_raw = {}, {}, {}, {}
+        grouped = {}
 
         sources = {"cu": (cu_hbm, 0), "i": (z_hbm, 0), "c": (c_hbm, 0), "f": (z_hbm, 1), "g0": (g0_hbm, 0),
                    "o": (z_hbm, 2), "g1": (g1_hbm, 0)}
 
         def load_step(n, names):
-            half, g = divmod(n, GROUPS)
-            cols = slice(HALF * half, HALF * (half + 1))
+            g, half = STEP_ORDER[n]
             for name in names:
                 src, gate = sources[name]
                 dtype = F32 if src is z_hbm else BF16
                 pool = four if name == "f" else three
-                t = pool.tile([P, 4, HALF], dtype, name=name, tag=name)
-                nc.sync.dma_start(out=t[:], in_=src[g][:, :, D * gate + cols.start:D * gate + cols.stop])
-                st[n][name] = t
+                steps[n][name] = pool.tile([P, 4, HALF], dtype, name=name, tag=name)
+                col = D * gate + HALF * half
+                nc.sync.dma_start(out=steps[n][name][:], in_=src[g][:, :, col:col + HALF])
 
         def load_h(g):
             h_raw[g] = two.tile([P, 4, D], BF16, name="h_raw", tag="h_raw")
             nc.sync.dma_start(out=h_raw[g][:], in_=h_hbm[g])
 
-        def load_r(s):
-            r_raw[s] = three.tile([P, 4, D], BF16, name="r_raw", tag="out_stage")
-            if s == PASS_O:
-                nc.sync.dma_start(out=r_raw[s][:], in_=r_hbm[:, :, 2 * D:3 * D])
+        def load_r(k_pass):
+            r_raw[k_pass] = three.tile([P, 4, D], BF16, name="r_raw", tag="r_raw")
+            if k_pass == PASS_O:
+                nc.sync.dma_start(out=r_raw[k_pass][:], in_=r_hbm[:, :, 2 * D:3 * D])
             else:
                 for gate in range(2):
-                    first = D * gate + HALF * s
-                    nc.sync.dma_start(out=r_raw[s][:, :, HALF * gate:HALF * (gate + 1)],
-                                      in_=r_hbm[:, :, first:first + HALF])
+                    col = D * gate + HALF * k_pass
+                    nc.sync.dma_start(out=r_raw[k_pass][:, :, HALF * gate:HALF * (gate + 1)],
+                                      in_=r_hbm[:, :, col:col + HALF])
 
         def tanh_a(n):
-            st[n]["a"] = three.tile([P, 4, HALF], F32, name="a", tag="a")
-            nc.scalar.activation(out=st[n]["a"][:], in_=st[n]["cu"][:], func=ACT.Tanh)
+            steps[n]["a"] = three.tile([P, 4, HALF], F32, name="a", tag="a")
+            nc.scalar.activation(out=steps[n]["a"][:], in_=steps[n]["cu"][:], func=ACT.Tanh)
 
         def sigmoid(n, gate):
-            nc.scalar.activation(out=st[n][gate][:], in_=st[n][gate][:], func=ACT.Sigmoid)
+            nc.scalar.activation(out=steps[n][gate][:], in_=steps[n][gate][:], func=ACT.Sigmoid)
 
         def i_times_a(n, engine):
-            s = st[n]
-            engine.tensor_tensor(out=s["a"][:], in0=s["i"][:], in1=s["a"][:], op=ALU.mult)
+            step = steps[n]
+            engine.tensor_tensor(out=step["a"][:], in0=step["i"][:], in1=step["a"][:], op=ALU.mult)
 
         def f_times_c(n, engine, out):
-            s = st[n]
-            s["fc"] = out
-            engine.tensor_tensor(out=out[:], in0=s["f"][:], in1=s["c"][:], op=ALU.mult)
+            step = steps[n]
+            step["fc"] = out
+            engine.tensor_tensor(out=out[:], in0=step["f"][:], in1=step["c"][:], op=ALU.mult)
 
         def g0_times_o(n, engine, rows):
-            s = st[n]
-            if "g0o" not in s:
-                s["g0o"] = two.tile([P, 4, HALF], F32, name="g0o", tag="g0o")
-            engine.tensor_tensor(out=s["g0o"][:, rows], in0=s["o"][:, rows], in1=s["g0"][:, rows], op=ALU.mult)
+            step = steps[n]
+            if "g0o" not in step:
+                step["g0o"] = two.tile([P, 4, HALF], F32, name="g0o", tag="g0o")
+            engine.tensor_tensor(out=step["g0o"][:, rows], in0=step["o"][:, rows], in1=step["g0"][:, rows],
+                                 op=ALU.mult)
 
         def gpsimd_products(n):
-            f_times_c(n + 1, nc.gpsimd, st[n]["f"])
+            f_times_c(n + 1, nc.gpsimd, steps[n]["f"])
             if n >= 1:
                 i_times_a(n + 1, nc.gpsimd)
             g0_times_o(n + 1, nc.gpsimd, slice(0, GPSIMD_ROWS if n >= 1 else 4))
 
-        def minus_one_times(out, gate, other):
-            nc.vector.scalar_tensor_tensor(out=out, in0=gate, scalar=1.0, in1=other, op0=ALU.subtract, op1=ALU.mult)
+        def minus_one_times(out, factor, other):
+            nc.vector.scalar_tensor_tensor(out=out, in0=factor, scalar=1.0, in1=other, op0=ALU.subtract,
+                                           op1=ALU.mult)
 
         def slope_o(n):
-            s = st[n]
-            minus_one_times(s["o"][:], s["o"][:], s["g0o"][:])
+            step = steps[n]
+            minus_one_times(step["o"][:], step["o"][:], step["g0o"][:])
 
         def slope_f(n):
-            s = st[n]
-            minus_one_times(s["fc"][:], s["f"][:], s["fc"][:])
+            step = steps[n]
+            minus_one_times(step["fc"][:], step["f"][:], step["fc"][:])
 
         def slope_i(n):
-            s = st[n]
-            minus_one_times(s["a"][:], s["i"][:], s["a"][:])
+            step = steps[n]
+            minus_one_times(step["a"][:], step["i"][:], step["a"][:])
 
         def new_cell_transposed(n):
-            s = st[n]
-            s["cn"] = []
+            step = steps[n]
+            step["cn_ps"] = []
             for q in range(2):
                 b = bank(CELL_BANKS[q])
                 for j in range(4):
-                    for k, term in enumerate(("a", "fc")):
-                        nc.tensor.matmul(out=b[:, P * j:P * (j + 1)], lhsT=s[term][:, j, P * q:P * (q + 1)],
-                                         rhs=ident[:], start=(k == 0), stop=(k == 1), is_transpose=True)
-                s["cn"].append(b)
+                    for term in ("a", "fc"):
+                        nc.tensor.matmul(out=b[:, P * j:P * (j + 1)], lhsT=step[term][:, j, P * q:P * (q + 1)],
+                                         rhs=ident[:], start=(term == "a"), stop=(term == "fc"), is_transpose=True)
+                step["cn_ps"].append(b)
 
         def tanh_and_square(n):
-            s = st[n]
-            s["ntc"] = [two.tile([P, 512], F32, name="ntc", tag="ntc") for q in range(2)]
-            s["sq"] = [two.tile([P, 512], F32, name="sq", tag="sq") for q in range(2)]
+            step = steps[n]
+            step["ntc"] = [two.tile([P, 512], F32, name="ntc", tag="ntc") for q in range(2)]
+            step["sq"] = [two.tile([P, 512], F32, name="sq", tag="sq") for q in range(2)]
             for q in range(2):
-                nc.scalar.activation(out=s["ntc"][q][:], in_=s["cn"][q][:], func=ACT.Tanh, scale=-1.0)
+                nc.scalar.activation(out=step["ntc"][q][:], in_=step["cn_ps"][q][:], func=ACT.Tanh, scale=-1.0)
             for q in range(2):
-                nc.scalar.activation(out=s["sq"][q][:], in_=s["ntc"][q][:], func=ACT.Square)
+                nc.scalar.activation(out=step["sq"][q][:], in_=step["ntc"][q][:], func=ACT.Square)
 
-        def transpose_back(src, k):
-            b = bank(k)
+        def transpose_back(src, bank_number):
+            b = bank(bank_number)
             for j in range(4):
                 nc.tensor.transpose(b[:, P * j:P * (j + 1)], src[:, P * j:P * (j + 1)], ident[:])
             return b[:].rearrange("p (j c) -> p j c", j=4)
 
         def tanh_back(n):
-            st[n]["ntc_ps"] = [transpose_back(st[n]["ntc"][q], CELL_BANKS[q]) for q in range(2)]
+            steps[n]["ntc_ps"] = [transpose_back(steps[n]["ntc"][q], CELL_BANKS[q]) for q in range(2)]
 
         def g0o_transposed(n):
-            s = st[n]
-            s["g0o_ps"] = []
+            step = steps[n]
+            step["g0o_ps"] = []
             for q in range(2):
                 b = bank(GRAD_BANKS[q])
                 for j in range(4):
-                    nc.tensor.transpose(b[:, P * j:P * (j + 1)], s["g0o"][:, j, P * q:P * (q + 1)], ident[:])
-                s["g0o_ps"].append(b)
+                    nc.tensor.transpose(b[:, P * j:P * (j + 1)], step["g0o"][:, j, P * q:P * (q + 1)], ident[:])
+                step["g0o_ps"].append(b)
 
         def g1_transposed(n):
-            s = st[n]
-            s["g1_ps"] = psum.tile([P, 2, 512], BF16, name="g1_bank", tag="bank%d" % G1_BANK)
+            step = steps[n]
+            step["g1_ps"] = psum.tile([P, 2, 512], BF16, name="g1_bank", tag="bank%d" % G1_BANK)
             for q in range(2):
                 for j in range(4):
-                    nc.tensor.transpose(s["g1_ps"][:, q, P * j:P * (j + 1)], s["g1"][:, j, P * q:P * (q + 1)],
-                                        ident_bf[:])
+                    nc.tensor.transpose(step["g1_ps"][:, q, P * j:P * (j + 1)],
+                                        step["g1"][:, j, P * q:P * (q + 1)], ident_bf[:])
 
-        def rounded_product(dz, first, count, in0, in1):
-            out = dz[:].rearrange("p (t m j) -> p m j t", t=4, j=4)[:, first:first + count]
+        def rounded_product(dz, first_m, count, in0, in1):
+            out = dz[:].rearrange("p (t m j) -> p m j t", t=4, j=4)[:, first_m:first_m + count]
             nc.vector.tensor_tensor(out=out, in0=in0.rearrange("p j (m t) -> p m j t", t=4),
                                     in1=in1.rearrange("p j (m t) -> p m j t", t=4), op=ALU.mult)
 
         def psum_products(n):
-            half, g = divmod(n, GROUPS)
-            s = st[n]
+            g, half = STEP_ORDER[n]
+            step = steps[n]
+            if half == 0:
+                dz_o[g] = two.tile([P, 2048], BF16, name="dz_o", tag="dz_o", align_bytes=64)
             for q in range(2):
-                minus_one_times(s["sq"][q][:], s["sq"][q][:], s["g0o_ps"][q][:])
+                minus_one_times(step["sq"][q][:], step["sq"][q][:], step["g0o_ps"][q][:])
             for q in range(2):
-                nc.vector.tensor_tensor(out=s["sq"][q][:], in0=s["sq"][q][:], in1=s["g1_ps"][:, q, :],
+                nc.vector.tensor_tensor(out=step["sq"][q][:], in0=step["sq"][q][:], in1=step["g1_ps"][:, q, :],
                                         op=ALU.subtract)
-            ndc_ps = [transpose_back(s["sq"][q], GRAD_BANKS[q]) for q in range(2)]
+            ndc_ps = [transpose_back(step["sq"][q], GRAD_BANKS[q]) for q in range(2)]
             for q in range(2):
-                rounded_product(dz_o[g], 64 * half + 32 * q, 32, s["ntc_ps"][q], s["o"][:, :, P * q:P * (q + 1)])
-            s["dz"] = two.tile([P, 2048], BF16, name="dz_if", tag="dz_if", align_bytes=64)
+                rounded_product(dz_o[g], 64 * half + 32 * q, 32, step["ntc_ps"][q],
+                                step["o"][:, :, P * q:P * (q + 1)])
+            step["dz_if"] = two.tile([P, 2048], BF16, name="dz_if", tag="dz_if", align_bytes=64)
             for q in range(2):
                 for gate, slope in enumerate(("a", "fc")):
-                    rounded_product(s["dz"], 64 * gate + 32 * q, 32, ndc_ps[q], s[slope][:, :, P * q:P * (q + 1)])
-
-        def last_step_tanh(n):
-            s = st[n]
-            s["ntc"] = three.tile([P, 4, HALF], F32, name="last_ntc", tag="a")
-            s["sq"] = three.tile([P, 4, HALF], F32, name="last_sq", tag="i")
-            nc.vector.tensor_tensor(out=s["ntc"][:], in0=s["a"][:], in1=s["fc"][:], op=ALU.add)
-            nc.scalar.activation(out=s["ntc"][:], in_=s["ntc"][:], func=ACT.Tanh, scale=-1.0)
-
-        def minus_dc(n):
-            s = st[n]
-            nc.vector.tensor_tensor(out=s["g0o"][:], in0=s["g0o"][:], in1=s["g1"][:], op=ALU.subtract)
-
-        def dz_i_and_f(n):
-            s = st[n]
-            s["dz"] = two.tile([P, 2048], BF16, name="dz_if", tag="dz_if", align_bytes=64)
-            rounded_product(s["dz"], 0, 64, s["a"][:], s["g0o"][:])
-            rounded_product(s["dz"], 64, 64, s["fc"][:], s["g0o"][:])
+                    rounded_product(step["dz_if"], 64 * gate + 32 * q, 32, ndc_ps[q],
+                                    step[slope][:, :, P * q:P * (q + 1)])
 
         def transpose_dz(dz):
             words = dz[:].bitcast(F32)
@@ -243,105 +231,104 @@ def tile_rlstmcell_pb_v_kernel(tc, inputs, h_state, c_state, c_upd, kernel, recu
                 banks.append(b)
             return banks
 
-        def group_features(key, tag, banks, second_engine_copy):
+        def group_features(key, tag, banks, second_copy):
             grouped[key] = two.tile([P, 2048], BF16, name=tag, tag=tag, align_bytes=64)
-            for u, copy in enumerate((nc.scalar.copy, second_engine_copy)):
+            for u, copy in enumerate((nc.scalar.copy, second_copy)):
                 out = grouped[key][:, 1024 * u:1024 * (u + 1)].rearrange("m (e p t) -> m e p t", e=2, t=4)
                 copy(out=out, in_=banks[u][:].bitcast(BF16).rearrange("m (t p e) -> m e p t", t=4, e=2))
 
         def group_h(g):
-            grouped["h", g] = two.tile([P, 2048], BF16, name="stage_o", tag="stage_o", align_bytes=64)
+            grouped["h", g] = two.tile([P, 2048], BF16, name="stage_h", tag="stage_o", align_bytes=64)
             nc.scalar.copy(out=grouped["h", g][:].rearrange("p (c i j) -> p c j i", i=4, j=4),
                            in_=h_raw[g][:].rearrange("p j (c i) -> p c j i", i=4))
 
-        def transpose_r(s):
-            words = r_raw[s][:].rearrange("p a k -> p (a k)").bitcast(F32)
+        def transpose_r(k_pass):
+            words = r_raw[k_pass][:].rearrange("p a k -> p (a k)").bitcast(F32)
             banks = []
             for pair in range(2):
-                b = bank(DZT_BANKS[pair])
+                b = bank(SPARE_BANKS[pair])
                 for a in range(2):
                     for u in range(2):
-                        first = 256 * (2 * pair + a)
+                        word = 256 * (2 * pair + a)
                         nc.tensor.transpose(b[:, P * (2 * a + u):P * (2 * a + u + 1)],
-                                            words[:, first + u:first + 256:2], ident[:])
+                                            words[:, word + u:word + 256:2], ident[:])
                 banks.append(b)
             return banks
 
-        def group_r(s, banks):
-            grouped["r", s] = keep.tile([P, 2048], BF16, name="stage_r", tag="stage_r", align_bytes=64)
-            words = grouped["r", s][:].bitcast(F32)
+        def group_r(k_pass, banks):
+            grouped["r", k_pass] = keep.tile([P, 2048], BF16, name="stage_r", tag="stage_r", align_bytes=64)
+            words = grouped["r", k_pass][:].bitcast(F32)
             for pair in range(2):
                 nc.scalar.copy(out=words[:, 512 * pair:512 * (pair + 1)].rearrange("m (a d u) -> m a d u", a=2, u=2),
                                in_=banks[pair][:].rearrange("m (a u d) -> m a d u", a=2, u=2))
 
-        def dh_passes(g, j, b, passes):
-            for s in passes:
-                mx(b, feat_q[g, s], E5, j, r_q[s], E4, s == 0, s == 1)
+        def quantise_tokens(g, k_pass, dz):
+            tok_q[g, k_pass] = quantise(keep, "tok%d_%d" % (g, k_pass), dz, E5)
 
-        def dh_pair(g, pair, bank_numbers):
-            banks = [bank(k) for k in bank_numbers]
-            for e in range(2):
-                dh_passes(g, 2 * pair + e, banks[e], (0, PASS_O, 1))
-            return banks
+        def quantise_features_o(g):
+            feat_q[g, PASS_O] = quantise(two, "feat_o", grouped["o", g], E5)
 
-        def store_dh_pair(g, pair, banks):
-            for e in range(2):
-                store_dh_tile(g, 2 * pair + e, banks[e], nc.scalar.copy)
+        def quantise_features_if(n):
+            g, half = STEP_ORDER[n]
+            pool, name = (keep, "feat0_%d" % g) if half == 0 else (two, "feat1")
+            feat_q[g, half] = quantise(pool, name, grouped["if", n], E5)
 
-        def dr_passes(s, a, b, groups):
-            for g in groups:
-                mx(b, h_q[g], E4, a, tok_q[g, s], E5, g == 0, g == GROUPS - 1)
+        def dh_passes(g, j, b, k_passes):
+            for k_pass in k_passes:
+                mx(b, feat_q[g, k_pass], E5, j, r_q[k_pass], E4, k_pass == 0, k_pass == 1)
 
-        def dr_tile(s, a, k, groups):
-            b = bank(k)
-            dr_passes(s, a, b, groups)
+        def dh_tile(g, j, bank_number):
+            b = bank(bank_number)
+            dh_passes(g, j, b, (0, PASS_O, 1))
             return b
 
-        def store_dr_tile(s, a, b, copy):
-            stage = six.tile([P, D], F32, name="dr_stage", tag="out_tile")
-            copy(out=stage[:].rearrange("p (m t) -> p m t", t=4), in_=b[:].rearrange("p (t m) -> p m t", t=4))
-            if s == PASS_O:
-                nc.sync.dma_start(out=dr_hbm[a][:, 2, :], in_=stage[:])
-            else:
-                nc.sync.dma_start(out=dr_hbm[a][:, 0:2, HALF * s:HALF * (s + 1)],
-                                  in_=stage[:].rearrange("p (gate c) -> p gate c", gate=2))
-
         def store_dh_tile(g, j, b, copy):
-            stage = six.tile([P, D], F32, name="dh_stage", tag="out_tile")
+            stage = eight.tile([P, D], F32, name="dh_stage", tag="out_tile")
             copy(out=stage[:], in_=b[:])
             nc.sync.dma_start(out=dh_hbm[g][:, j, :], in_=stage[:])
 
-        def output_tile(g, k, bank_number):
-            if g == 0:
-                return dr_tile(0, k, bank_number, range(GROUPS))
+        def dr_passes(k_pass, a, b, groups):
+            for g in groups:
+                mx(b, h_q[g], E4, a, tok_q[g, k_pass], E5, g == 0, g == GROUPS - 1)
+
+        def dr_tile(k_pass, a, bank_number, groups):
             b = bank(bank_number)
-            dh_passes(g - 1, k, b, (0, PASS_O, 1))
+            dr_passes(k_pass, a, b, groups)
             return b
 
-        def store_output(g, k, b, copy):
-            if g == 0:
-                store_dr_tile(0, k, b, copy)
+        def store_dr_tile(k_pass, a, b, copy):
+            stage = eight.tile([P, D], F32, name="dr_stage", tag="out_tile")
+            copy(out=stage[:].rearrange("p (m t) -> p m t", t=4), in_=b[:].rearrange("p (t m) -> p m t", t=4))
+            if k_pass == PASS_O:
+                nc.sync.dma_start(out=dr_hbm[a][:, 2, :], in_=stage[:])
             else:
-                store_dh_tile(g - 1, k, b, copy)
+                nc.sync.dma_start(out=dr_hbm[a][:, 0:2, HALF * k_pass:HALF * (k_pass + 1)],
+                                  in_=stage[:].rearrange("p (gate c) -> p gate c", gate=2))
 
-        def quantise_features_if(n):
-            half, g = divmod(n, GROUPS)
-            pool, name = (keep, "feat0_%d" % g) if half == 0 else (two, "feat1")
-            feat_q[g, half] = quantise(pool, name, grouped["if", n], E5)
+        def output_tile(n, number, bank_number):
+            if n == FIRST_HALVES_DONE:
+                return dr_tile(0, number, bank_number, range(GROUPS))
+            return dh_tile(n - FIRST_OUTPUT_STEP, number, bank_number)
+
+        def store_output(n, number, b, copy):
+            if n == FIRST_HALVES_DONE:
+                store_dr_tile(0, number, b, copy)
+            else:
+                store_dh_tile(n - FIRST_OUTPUT_STEP, number, b, copy)
 
         s_copy, v_copy = nc.scalar.copy, nc.vector.tensor_copy
 
         ctx.enter_context(tc.manual_schedule())
-        nc.scalar.activation(out=warm[:], in_=ident[:, 0:8], func=ACT.Sigmoid)
+
         first_fc = four.tile([P, 4, HALF], F32, name="first_fc", tag="f")
-        load_step(0, ("cu", "i", "c", "f", "g0", "o", "g1"))
+        load_step(0, ("i", "cu", "f", "c", "o", "g0", "g1"))
         load_step(1, ("cu", "i", "c", "f", "g0", "o", "g1"))
-        load_step(2, ("cu", "i"))
         load_h(0)
-        load_step(2, ("c", "f", "g0", "o", "g1"))
-        load_h(1)
+        load_step(2, ("cu", "i", "c", "f", "g0", "o", "g1"))
+        load_r(0)
+        sigmoid(0, "i")
         tanh_a(0)
-        for gate in ("i", "f", "o"):
+        for gate in ("f", "o"):
             sigmoid(0, gate)
         i_times_a(0, nc.vector)
         f_times_c(0, nc.vector, first_fc)
@@ -359,59 +346,65 @@ def tile_rlstmcell_pb_v_kernel(tc, inputs, h_state, c_state, c_upd, kernel, recu
         slope_f(0)
         i_times_a(1, nc.vector)
 
-        all_groups, early_groups, last_group = range(GROUPS), range(GROUPS - 1), (GROUPS - 1,)
         outputs = {}
         for n in range(STEPS - 2):
-            half, g = divmod(n, GROUPS)
-            with_r = 2 <= n < 5
+            g, half = STEP_ORDER[n]
+            with_r = 1 <= n <= FIRST_OUTPUT_STEP
             sigmoid(n + 1, "o")
             gpsimd_products(n)
-            if with_r:
-                group_r(n - 2, transpose_r(n - 2))
-            if n > GROUPS:
-                outputs[3] = output_tile(g - 1, 3, ACC_BANKS[1])
             psum_products(n)
+            if n > FIRST_OUTPUT_STEP:
+                outputs[3] = output_tile(n - 1, 3, SPARE_BANKS[1])
+            if with_r:
+                r_banks = transpose_r(n - 1)
             if half == 1:
                 o_banks = transpose_dz(dz_o[g])
-                if g >= 1:
-                    outputs[2] = output_tile(g - 1, 2, ACC_BANKS[0])
-                    store_output(g - 1, 3, outputs[3], v_copy)
             else:
                 group_h(g)
-                if g + 2 < GROUPS:
-                    load_h(g + 2)
+            if n > FIRST_OUTPUT_STEP:
+                outputs[2] = output_tile(n - 1, 2, SPARE_BANKS[0])
+                store_output(n - 1, 3, outputs[3], v_copy)
             tanh_a(n + 2)
             sigmoid(n + 2, "i")
+            if with_r:
+                group_r(n - 1, r_banks)
             if half == 1:
                 group_features(("o", g), "stage_o", o_banks, s_copy)
-            if n > GROUPS:
-                store_output(g - 1, 2, outputs[2], s_copy)
+            if n > FIRST_OUTPUT_STEP:
+                store_output(n - 1, 2, outputs[2], s_copy)
             new_cell_transposed(n + 1)
+            if 1 <= n < GROUPS:
+                load_h(n)
             if n + 3 < STEPS:
-                load_step(n + 3, sources)
-            if n < 3:
-                load_r(n)
-            if 1 <= n:
+                load_step(n + 3, ("cu", "i"))
+            if n + 1 <= PASS_O:
+                load_r(n + 1)
+            if n + 3 < STEPS:
+                load_step(n + 3, ("c", "f", "g0", "o", "g1"))
+            if n >= 1:
                 quantise_features_if(n - 1)
-                g0_times_o(n + 1, nc.vector, slice(GPSIMD_ROWS, 4))
-            if half == 1:
-                for k in range(2):
-                    outputs[k] = output_tile(g, k, GRAD_BANKS[k])
-            if_banks = transpose_dz(st[n]["dz"])
-            tanh_and_square(n + 1)
-            if with_r:
-                r_q[n - 2] = quantise(keep, "r%d" % (n - 2), grouped["r", n - 2], E4)
-            tok_q[g, half] = quantise(keep, "tok%d_%d" % (g, half), st[n]["dz"], E5)
-            if half == 1:
-                tok_q[g, PASS_O] = quantise(keep, "tok%d_o" % g, dz_o[g], E5)
-                feat_q[g, PASS_O] = quantise(two, "feat_o", grouped["o", g], E5)
-                for k in range(2):
-                    store_output(g, k, outputs[k], s_copy)
-            else:
+            if half == 0:
                 h_q[g] = quantise(keep, "h%d" % g, grouped["h", g], E4)
+            else:
+                quantise_tokens(g, PASS_O, dz_o[g])
+            if n >= 1:
+                g0_times_o(n + 1, nc.vector, slice(GPSIMD_ROWS, 4))
+            quantise_tokens(g, half, steps[n]["dz_if"])
+            if with_r:
+                r_q[n - 1] = quantise(keep, "r%d" % (n - 1), grouped["r", n - 1], E4)
+            if n >= FIRST_OUTPUT_STEP:
+                for number in range(2):
+                    outputs[number] = output_tile(n, number, GRAD_BANKS[number])
+            if half == 1:
+                quantise_features_o(g)
+            if_banks = transpose_dz(steps[n]["dz_if"])
+            tanh_and_square(n + 1)
+            if n >= FIRST_OUTPUT_STEP:
+                for number in range(2):
+                    store_output(n, number, outputs[number], s_copy)
             g0o_transposed(n + 1)
-            tanh_back(n + 1)
             g1_transposed(n + 1)
+            tanh_back(n + 1)
             slope_o(n + 1)
             slope_f(n + 1)
             slope_i(n + 1)
@@ -419,67 +412,72 @@ def tile_rlstmcell_pb_v_kernel(tc, inputs, h_state, c_state, c_upd, kernel, recu
             group_features(("if", n), "stage_if", if_banks, s_copy)
 
         n, g = STEPS - 2, GROUPS - 2
-        s = st[n + 1]
+        last = steps[n + 1]
         sigmoid(n + 1, "o")
         gpsimd_products(n)
-        outputs[3] = output_tile(g - 1, 3, ACC_BANKS[1])
         psum_products(n)
+        outputs[3] = output_tile(n - 1, 3, SPARE_BANKS[1])
         o_banks = transpose_dz(dz_o[g])
-        outputs[2] = output_tile(g - 1, 2, ACC_BANKS[0])
-        store_output(g - 1, 3, outputs[3], v_copy)
+        outputs[2] = output_tile(n - 1, 2, SPARE_BANKS[0])
+        o_tiles = [dr_tile(PASS_O, a, CELL_BANKS[a], range(g)) for a in range(2)]
+        store_output(n - 1, 3, outputs[3], v_copy)
         group_features(("o", g), "stage_o", o_banks, s_copy)
-        store_output(g - 1, 2, outputs[2], s_copy)
-        quantise_features_if(n - 1)
-        early_dh = dh_pair(g - 1, 0, CELL_BANKS)
-        if_banks = transpose_dz(st[n]["dz"])
-        late_dh = dh_pair(g - 1, 1, GRAD_BANKS)
-        last_step_tanh(n + 1)
-        tok_q[g, 1] = quantise(keep, "tok%d_1" % g, st[n]["dz"], E5)
-        tok_q[g, PASS_O] = quantise(keep, "tok%d_o" % g, dz_o[g], E5)
+        store_output(n - 1, 2, outputs[2], s_copy)
+        if_banks = transpose_dz(steps[n]["dz_if"])
+        o_tiles.extend([dr_tile(PASS_O, 2 + a, GRAD_BANKS[a], range(g)) for a in range(2)])
+        last_ntc = three.tile([P, 4, HALF], F32, name="last_ntc", tag="a")
+        last_sq = three.tile([P, 4, HALF], F32, name="last_sq", tag="i")
+        nc.vector.tensor_tensor(out=last_ntc[:], in0=last["a"][:], in1=last["fc"][:], op=ALU.add)
+        nc.scalar.activation(out=last_ntc[:], in_=last_ntc[:], func=ACT.Tanh, scale=-1.0)
+        quantise_tokens(g, PASS_O, dz_o[g])
+        quantise_tokens(g, 1, steps[n]["dz_if"])
         g0_times_o(n + 1, nc.vector, slice(GPSIMD_ROWS, 4))
-        feat_q[g, PASS_O] = quantise(two, "feat_o", grouped["o", g], E5)
-        store_dh_pair(g - 1, 0, early_dh)
+        quantise_features_o(g)
+        quantise_features_if(n - 1)
         group_features(("if", n), "stage_if", if_banks, s_copy)
-        nc.scalar.activation(out=s["sq"][:], in_=s["ntc"][:], func=ACT.Square)
-        store_dh_pair(g - 1, 1, late_dh)
-        if_tiles = [dr_tile(1, a, ACC_BANKS[a], early_groups) for a in range(2)]
-        o_tiles = [dr_tile(PASS_O, a, a, early_groups) for a in range(2)]
+        nc.scalar.activation(out=last_sq[:], in_=last_ntc[:], func=ACT.Square)
+        for a in range(4):
+            dr_passes(PASS_O, a, o_tiles[a], (g,))
+        if_tiles = [dr_tile(1, a, SPARE_BANKS[a], range(g + 1)) for a in range(2)]
 
         n, g = STEPS - 1, GROUPS - 1
         slope_o(n)
         slope_i(n)
+        rounded_product(dz_o[g], 64, 64, last_ntc[:], last["o"][:])
         quantise_features_if(n - 1)
-        early_dh = dh_pair(g - 1, 0, DZT_BANKS)
-        o_tiles.extend([dr_tile(PASS_O, a, a, early_groups) for a in range(2, 4)])
-        rounded_product(dz_o[g], 64, 64, s["ntc"][:], s["o"][:])
-        minus_one_times(s["g0o"][:], s["sq"][:], s["g0o"][:])
-        tok_q[g, PASS_O] = quantise(keep, "tok%d_o" % g, dz_o[g], E5)
+        dh_before = [dh_tile(g - 1, j, DZT_BANKS[j]) for j in range(2)]
+        quantise_tokens(g, PASS_O, dz_o[g])
         for a in range(4):
-            dr_passes(PASS_O, a, o_tiles[a], last_group)
-        store_dh_pair(g - 1, 0, early_dh)
+            dr_passes(PASS_O, a, o_tiles[a], (g,))
+        for j in range(2):
+            store_dh_tile(g - 1, j, dh_before[j], s_copy)
         o_banks = transpose_dz(dz_o[g])
         for a in range(4):
             store_dr_tile(PASS_O, a, o_tiles[a], s_copy)
-        late_dh = dh_pair(g - 1, 1, CELL_BANKS)
-        if_tiles.extend([dr_tile(1, 2 + a, GRAD_BANKS[a], early_groups) for a in range(2)])
+        dh_before.extend([dh_tile(g - 1, 2 + e, CELL_BANKS[e]) for e in range(2)])
+        if_tiles.extend([dr_tile(1, 2 + a, GRAD_BANKS[a], range(g)) for a in range(2)])
         group_features(("o", g), "stage_o", o_banks, s_copy)
-        minus_dc(n)
+        last_ndc = last["g0o"]
+        minus_one_times(last_ndc[:], last_sq[:], last["g0o"][:])
         slope_f(n)
-        dz_i_and_f(n)
-        if_banks = transpose_dz(s["dz"])
-        store_dh_tile(g - 1, 2, late_dh[0], v_copy)
-        tok_q[g, 1] = quantise(keep, "tok%d_1" % g, s["dz"], E5)
-        store_dh_tile(g - 1, 3, late_dh[1], s_copy)
-        feat_q[g, PASS_O] = quantise(two, "feat_o", grouped["o", g], E5)
+        nc.vector.tensor_tensor(out=last_ndc[:], in0=last_ndc[:], in1=last["g1"][:], op=ALU.subtract)
+        last_dz_if = two.tile([P, 2048], BF16, name="dz_if", tag="dz_if", align_bytes=64)
+        for gate, slope in enumerate(("a", "fc")):
+            rounded_product(last_dz_if, 64 * gate, 64, last[slope][:], last_ndc[:])
+        if_banks = transpose_dz(last_dz_if)
+        for j in range(2, 4):
+            store_dh_tile(g - 1, j, dh_before[j], s_copy)
+        quantise_features_o(g)
+        quantise_tokens(g, 1, last_dz_if)
         for a in range(4):
-            dr_passes(1, a, if_tiles[a], last_group)
+            dr_passes(1, a, if_tiles[a], (g,))
         group_features(("if", n), "stage_if", if_banks, v_copy)
         quantise_features_if(n)
-        dh_banks = [bank(k) for k in CELL_BANKS + DZT_BANKS]
+        dh_banks = [bank(number) for number in CELL_BANKS + DZT_BANKS]
         for pair in range(2):
-            for passes in ((0, PASS_O), (1,)):
+            for k_passes in ((0, PASS_O), (1,)):
                 for j in (2 * pair, 2 * pair + 1):
-                    dh_passes(g, j, dh_banks[j], passes)
+                    dh_passes(g, j, dh_banks[j], k_passes)
         for a, copy in enumerate((s_copy, s_copy, v_copy, s_copy)):
             store_dr_tile(1, a, if_tiles[a], copy)
         for j, copy in enumerate((v_copy, s_copy, v_copy, s_copy)):

from contextlib import ExitStack

import concourse.mybir as mybir
from concourse.masks import make_identity

T, D = 2048, 512
FLOPS = 2 * 2 * T * D * 3 * D
BYTES = T * 3 * D * 4 + 5 * T * D * 2 + D * 3 * D * 2 + T * D * 4 + D * 3 * D * 4

F32 = mybir.dt.float32
BF16 = mybir.dt.bfloat16
U32 = mybir.dt.uint32
U8 = mybir.dt.uint8
E4 = mybir.dt.float8_e4m3fn_x4
E5 = mybir.dt.float8_e5m2_x4
ACT = mybir.ActivationFunctionType
ALU = mybir.AluOpType

P = 128
GROUPS = T // 512
HALF = D // 2
PASS_O = 2
STEP_ORDER = ((0, 0), (0, 1), (1, 0), (1, 1), (2, 0), (3, 0), (2, 1), (3, 1))
STEPS = len(STEP_ORDER)
FIRST_OUTPUT_STEP = 3
FIRST_HALVES_DONE = 5
CELL_BANKS = (0, 1)
GRAD_BANKS = (2, 3)
DZT_BANKS = (4, 5)
SPARE_BANKS = (6, 7)
G1_BANK = 6
GPSIMD_ROWS = 2


def tile_rlstmcell_pb_v_kernel(tc, inputs, h_state, c_state, c_upd, kernel, recurrent_kernel, bias,
                                            z, grad_0, grad_1, out_0, out_1):
    nc = tc.nc

    def by_token(ap):
        return ap.rearrange("b (s d) -> (b s) d", d=D).rearrange("(g p j) d -> g p j d", p=P, j=4)

    h_hbm, c_hbm, g0_hbm, g1_hbm, dh_hbm = (by_token(ap) for ap in (h_state, c_state, grad_0, grad_1, out_0))
    cu_hbm = c_upd.rearrange("b s d -> (b s) d").rearrange("(g p j) d -> g p j d", p=P, j=4)
    z_hbm = z.rearrange("b s k -> (b s) k").rearrange("(g p j) k -> g p j k", p=P, j=4)
    r_hbm = recurrent_kernel.rearrange("(a p) k -> p a k", p=P)
    dr_hbm = out_1.rearrange("(a p) (gate c) -> a p gate c", p=P, gate=3)

    with ExitStack() as ctx:
        keep = ctx.enter_context(tc.tile_pool(name="keep", bufs=1))
        two = ctx.enter_context(tc.tile_pool(name="two", bufs=2))
        three = ctx.enter_context(tc.tile_pool(name="three", bufs=3))
        four = ctx.enter_context(tc.tile_pool(name="four", bufs=4))
        eight = ctx.enter_context(tc.tile_pool(name="eight", bufs=8))
        psum = ctx.enter_context(tc.psum_pool(name="psum", bufs=1))

        ident = keep.tile([P, P], F32, name="ident")
        make_identity(nc, ident[:])
        ident_bf = keep.tile([P, P], BF16, name="ident_bf")
        make_identity(nc, ident_bf[:])

        def bank(number):
            return psum.tile([P, 512], F32, name="bank%d" % number, tag="bank%d" % number)

        def quantise(pool, name, src, fmt):
            codes = pool.tile([P, 512], U32, name=name + "_codes", tag=name + "_codes", align_bytes=64)
            scales = pool.tile([P, 512], U8, name=name + "_scales", tag=name + "_scales", align_bytes=64)
            nc.vector.quantize_mx(out=codes[:].bitcast(fmt), scales=scales[:], in_=src[:])
            return codes, scales

        def mx(out, lhs, lhs_fmt, lhs_tile, rhs, rhs_fmt, start, stop):
            cols = slice(P * lhs_tile, P * (lhs_tile + 1))
            nc.tensor.matmul_mx(out=out[:], lhsT=lhs[0][:, cols].bitcast(lhs_fmt), lhsT_scale=lhs[1][:, cols],
                                rhs=rhs[0][:].bitcast(rhs_fmt), rhs_scale=rhs[1][:], start=start, stop=stop)

        steps = [dict() for n in range(STEPS)]
        dz_o = {}
        tok_q, feat_q = {}, {}
        h_q, r_q, h_raw, r_raw = {}, {}, {}, {}
        grouped = {}

        sources = {"cu": (cu_hbm, 0), "i": (z_hbm, 0), "c": (c_hbm, 0), "f": (z_hbm, 1), "g0": (g0_hbm, 0),
                   "o": (z_hbm, 2), "g1": (g1_hbm, 0)}

        def load_step(n, names):
            g, half = STEP_ORDER[n]
            for name in names:
                src, gate = sources[name]
                dtype = F32 if src is z_hbm else BF16
                pool = four if name == "f" else three
                steps[n][name] = pool.tile([P, 4, HALF], dtype, name=name, tag=name)
                col = D * gate + HALF * half
                nc.sync.dma_start(out=steps[n][name][:], in_=src[g][:, :, col:col + HALF])

        def load_h(g):
            h_raw[g] = two.tile([P, 4, D], BF16, name="h_raw", tag="h_raw")
            nc.sync.dma_start(out=h_raw[g][:], in_=h_hbm[g])

        def load_r(k_pass):
            r_raw[k_pass] = three.tile([P, 4, D], BF16, name="r_raw", tag="r_raw")
            if k_pass == PASS_O:
                nc.sync.dma_start(out=r_raw[k_pass][:], in_=r_hbm[:, :, 2 * D:3 * D])
            else:
                for gate in range(2):
                    col = D * gate + HALF * k_pass
                    nc.sync.dma_start(out=r_raw[k_pass][:, :, HALF * gate:HALF * (gate + 1)],
                                      in_=r_hbm[:, :, col:col + HALF])

        def tanh_a(n):
            steps[n]["a"] = three.tile([P, 4, HALF], F32, name="a", tag="a")
            nc.scalar.activation(out=steps[n]["a"][:], in_=steps[n]["cu"][:], func=ACT.Tanh)

        def sigmoid(n, gate):
            nc.scalar.activation(out=steps[n][gate][:], in_=steps[n][gate][:], func=ACT.Sigmoid)

        def i_times_a(n, engine):
            step = steps[n]
            engine.tensor_tensor(out=step["a"][:], in0=step["i"][:], in1=step["a"][:], op=ALU.mult)

        def f_times_c(n, engine, out):
            step = steps[n]
            step["fc"] = out
            engine.tensor_tensor(out=out[:], in0=step["f"][:], in1=step["c"][:], op=ALU.mult)

        def g0_times_o(n, engine, rows):
            step = steps[n]
            if "g0o" not in step:
                step["g0o"] = two.tile([P, 4, HALF], F32, name="g0o", tag="g0o")
            engine.tensor_tensor(out=step["g0o"][:, rows], in0=step["o"][:, rows], in1=step["g0"][:, rows],
                                 op=ALU.mult)

        def gpsimd_products(n):
            f_times_c(n + 1, nc.gpsimd, steps[n]["f"])
            if n >= 1:
                i_times_a(n + 1, nc.gpsimd)
            g0_times_o(n + 1, nc.gpsimd, slice(0, GPSIMD_ROWS if n >= 1 else 4))

        def minus_one_times(out, factor, other):
            nc.vector.scalar_tensor_tensor(out=out, in0=factor, scalar=1.0, in1=other, op0=ALU.subtract,
                                           op1=ALU.mult)

        def slope_o(n):
            step = steps[n]
            minus_one_times(step["o"][:], step["o"][:], step["g0o"][:])

        def slope_f(n):
            step = steps[n]
            minus_one_times(step["fc"][:], step["f"][:], step["fc"][:])

        def slope_i(n):
            step = steps[n]
            minus_one_times(step["a"][:], step["i"][:], step["a"][:])

        def new_cell_transposed(n):
            step = steps[n]
            step["cn_ps"] = []
            for q in range(2):
                b = bank(CELL_BANKS[q])
                for j in range(4):
                    for term in ("a", "fc"):
                        nc.tensor.matmul(out=b[:, P * j:P * (j + 1)], lhsT=step[term][:, j, P * q:P * (q + 1)],
                                         rhs=ident[:], start=(term == "a"), stop=(term == "fc"), is_transpose=True)
                step["cn_ps"].append(b)

        def tanh_and_square(n):
            step = steps[n]
            step["ntc"] = [two.tile([P, 512], F32, name="ntc", tag="ntc") for q in range(2)]
            step["sq"] = [two.tile([P, 512], F32, name="sq", tag="sq") for q in range(2)]
            for q in range(2):
                nc.scalar.activation(out=step["ntc"][q][:], in_=step["cn_ps"][q][:], func=ACT.Tanh, scale=-1.0)
            for q in range(2):
                nc.scalar.activation(out=step["sq"][q][:], in_=step["ntc"][q][:], func=ACT.Square)

        def transpose_back(src, bank_number):
            b = bank(bank_number)
            for j in range(4):
                nc.tensor.transpose(b[:, P * j:P * (j + 1)], src[:, P * j:P * (j + 1)], ident[:])
            return b[:].rearrange("p (j c) -> p j c", j=4)

        def tanh_back(n):
            steps[n]["ntc_ps"] = [transpose_back(steps[n]["ntc"][q], CELL_BANKS[q]) for q in range(2)]

        def g0o_transposed(n):
            step = steps[n]
            step["g0o_ps"] = []
            for q in range(2):
                b = bank(GRAD_BANKS[q])
                for j in range(4):
                    nc.tensor.transpose(b[:, P * j:P * (j + 1)], step["g0o"][:, j, P * q:P * (q + 1)], ident[:])
                step["g0o_ps"].append(b)

        def g1_transposed(n):
            step = steps[n]
            step["g1_ps"] = psum.tile([P, 2, 512], BF16, name="g1_bank", tag="bank%d" % G1_BANK)
            for q in range(2):
                for j in range(4):
                    nc.tensor.transpose(step["g1_ps"][:, q, P * j:P * (j + 1)],
                                        step["g1"][:, j, P * q:P * (q + 1)], ident_bf[:])

        def rounded_product(dz, first_m, count, in0, in1):
            out = dz[:].rearrange("p (t m j) -> p m j t", t=4, j=4)[:, first_m:first_m + count]
            nc.vector.tensor_tensor(out=out, in0=in0.rearrange("p j (m t) -> p m j t", t=4),
                                    in1=in1.rearrange("p j (m t) -> p m j t", t=4), op=ALU.mult)

        def psum_products(n):
            g, half = STEP_ORDER[n]
            step = steps[n]
            if half == 0:
                dz_o[g] = two.tile([P, 2048], BF16, name="dz_o", tag="dz_o", align_bytes=64)
            for q in range(2):
                minus_one_times(step["sq"][q][:], step["sq"][q][:], step["g0o_ps"][q][:])
            for q in range(2):
                nc.vector.tensor_tensor(out=step["sq"][q][:], in0=step["sq"][q][:], in1=step["g1_ps"][:, q, :],
                                        op=ALU.subtract)
            ndc_ps = [transpose_back(step["sq"][q], GRAD_BANKS[q]) for q in range(2)]
            for q in range(2):
                rounded_product(dz_o[g], 64 * half + 32 * q, 32, step["ntc_ps"][q],
                                step["o"][:, :, P * q:P * (q + 1)])
            step["dz_if"] = two.tile([P, 2048], BF16, name="dz_if", tag="dz_if", align_bytes=64)
            for q in range(2):
                for gate, slope in enumerate(("a", "fc")):
                    rounded_product(step["dz_if"], 64 * gate + 32 * q, 32, ndc_ps[q],
                                    step[slope][:, :, P * q:P * (q + 1)])

        def transpose_dz(dz):
            words = dz[:].bitcast(F32)
            banks = []
            for u in range(2):
                b = bank(DZT_BANKS[u])
                for t in range(4):
                    nc.tensor.transpose(b[:, P * t:P * (t + 1)], words[:, 256 * t + u:256 * (t + 1):2], ident[:])
                banks.append(b)
            return banks

        def group_features(key, tag, banks, second_copy):
            grouped[key] = two.tile([P, 2048], BF16, name=tag, tag=tag, align_bytes=64)
            for u, copy in enumerate((nc.scalar.copy, second_copy)):
                out = grouped[key][:, 1024 * u:1024 * (u + 1)].rearrange("m (e p t) -> m e p t", e=2, t=4)
                copy(out=out, in_=banks[u][:].bitcast(BF16).rearrange("m (t p e) -> m e p t", t=4, e=2))

        def group_h(g):
            grouped["h", g] = two.tile([P, 2048], BF16, name="stage_h", tag="stage_o", align_bytes=64)
            nc.scalar.copy(out=grouped["h", g][:].rearrange("p (c i j) -> p c j i", i=4, j=4),
                           in_=h_raw[g][:].rearrange("p j (c i) -> p c j i", i=4))

        def transpose_r(k_pass):
            words = r_raw[k_pass][:].rearrange("p a k -> p (a k)").bitcast(F32)
            banks = []
            for pair in range(2):
                b = bank(SPARE_BANKS[pair])
                for a in range(2):
                    for u in range(2):
                        word = 256 * (2 * pair + a)
                        nc.tensor.transpose(b[:, P * (2 * a + u):P * (2 * a + u + 1)],
                                            words[:, word + u:word + 256:2], ident[:])
                banks.append(b)
            return banks

        def group_r(k_pass, banks):
            grouped["r", k_pass] = keep.tile([P, 2048], BF16, name="stage_r", tag="stage_r", align_bytes=64)
            words = grouped["r", k_pass][:].bitcast(F32)
            for pair in range(2):
                nc.scalar.copy(out=words[:, 512 * pair:512 * (pair + 1)].rearrange("m (a d u) -> m a d u", a=2, u=2),
                               in_=banks[pair][:].rearrange("m (a u d) -> m a d u", a=2, u=2))

        def quantise_tokens(g, k_pass, dz):
            tok_q[g, k_pass] = quantise(keep, "tok%d_%d" % (g, k_pass), dz, E5)

        def quantise_features_o(g):
            feat_q[g, PASS_O] = quantise(two, "feat_o", grouped["o", g], E5)

        def quantise_features_if(n):
            g, half = STEP_ORDER[n]
            pool, name = (keep, "feat0_%d" % g) if half == 0 else (two, "feat1")
            feat_q[g, half] = quantise(pool, name, grouped["if", n], E5)

        def dh_passes(g, j, b, k_passes):
            for k_pass in k_passes:
                mx(b, feat_q[g, k_pass], E5, j, r_q[k_pass], E4, k_pass == 0, k_pass == 1)

        def dh_tile(g, j, bank_number):
            b = bank(bank_number)
            dh_passes(g, j, b, (0, PASS_O, 1))
            return b

        def store_dh_tile(g, j, b, copy):
            stage = eight.tile([P, D], F32, name="dh_stage", tag="out_tile")
            copy(out=stage[:], in_=b[:])
            nc.sync.dma_start(out=dh_hbm[g][:, j, :], in_=stage[:])

        def dr_passes(k_pass, a, b, groups):
            for g in groups:
                mx(b, h_q[g], E4, a, tok_q[g, k_pass], E5, g == 0, g == GROUPS - 1)

        def dr_tile(k_pass, a, bank_number, groups):
            b = bank(bank_number)
            dr_passes(k_pass, a, b, groups)
            return b

        def store_dr_tile(k_pass, a, b, copy):
            stage = eight.tile([P, D], F32, name="dr_stage", tag="out_tile")
            copy(out=stage[:].rearrange("p (m t) -> p m t", t=4), in_=b[:].rearrange("p (t m) -> p m t", t=4))
            if k_pass == PASS_O:
                nc.sync.dma_start(out=dr_hbm[a][:, 2, :], in_=stage[:])
            else:
                nc.sync.dma_start(out=dr_hbm[a][:, 0:2, HALF * k_pass:HALF * (k_pass + 1)],
                                  in_=stage[:].rearrange("p (gate c) -> p gate c", gate=2))

        def output_tile(n, number, bank_number):
            if n == FIRST_HALVES_DONE:
                return dr_tile(0, number, bank_number, range(GROUPS))
            return dh_tile(n - FIRST_OUTPUT_STEP, number, bank_number)

        def store_output(n, number, b, copy):
            if n == FIRST_HALVES_DONE:
                store_dr_tile(0, number, b, copy)
            else:
                store_dh_tile(n - FIRST_OUTPUT_STEP, number, b, copy)

        s_copy, v_copy = nc.scalar.copy, nc.vector.tensor_copy

        ctx.enter_context(tc.manual_schedule())

        first_fc = four.tile([P, 4, HALF], F32, name="first_fc", tag="f")
        load_step(0, ("i", "cu", "f", "c", "o", "g0", "g1"))
        load_step(1, ("cu", "i", "c", "f", "g0", "o", "g1"))
        load_h(0)
        load_step(2, ("cu", "i", "c", "f", "g0", "o", "g1"))
        load_r(0)
        sigmoid(0, "i")
        tanh_a(0)
        for gate in ("f", "o"):
            sigmoid(0, gate)
        i_times_a(0, nc.vector)
        f_times_c(0, nc.vector, first_fc)
        new_cell_transposed(0)
        g0_times_o(0, nc.vector, slice(0, 4))
        g0o_transposed(0)
        g1_transposed(0)
        tanh_a(1)
        tanh_and_square(0)
        tanh_back(0)
        sigmoid(1, "i")
        sigmoid(1, "f")
        slope_i(0)
        slope_o(0)
        slope_f(0)
        i_times_a(1, nc.vector)

        outputs = {}
        for n in range(STEPS - 2):
            g, half = STEP_ORDER[n]
            with_r = 1 <= n <= FIRST_OUTPUT_STEP
            sigmoid(n + 1, "o")
            gpsimd_products(n)
            psum_products(n)
            if n > FIRST_OUTPUT_STEP:
                outputs[3] = output_tile(n - 1, 3, SPARE_BANKS[1])
            if with_r:
                r_banks = transpose_r(n - 1)
            if half == 1:
                o_banks = transpose_dz(dz_o[g])
            else:
                group_h(g)
            if n > FIRST_OUTPUT_STEP:
                outputs[2] = output_tile(n - 1, 2, SPARE_BANKS[0])
                store_output(n - 1, 3, outputs[3], v_copy)
            tanh_a(n + 2)
            sigmoid(n + 2, "i")
            if with_r:
                group_r(n - 1, r_banks)
            if half == 1:
                group_features(("o", g), "stage_o", o_banks, s_copy)
            if n > FIRST_OUTPUT_STEP:
                store_output(n - 1, 2, outputs[2], s_copy)
            new_cell_transposed(n + 1)
            if 1 <= n < GROUPS:
                load_h(n)
            if n + 3 < STEPS:
                load_step(n + 3, ("cu", "i"))
            if n + 1 <= PASS_O:
                load_r(n + 1)
            if n + 3 < STEPS:
                load_step(n + 3, ("c", "f", "g0", "o", "g1"))
            if n >= 1:
                quantise_features_if(n - 1)
            if half == 0:
                h_q[g] = quantise(keep, "h%d" % g, grouped["h", g], E4)
            else:
                quantise_tokens(g, PASS_O, dz_o[g])
            if n >= 1:
                g0_times_o(n + 1, nc.vector, slice(GPSIMD_ROWS, 4))
            quantise_tokens(g, half, steps[n]["dz_if"])
            if with_r:
                r_q[n - 1] = quantise(keep, "r%d" % (n - 1), grouped["r", n - 1], E4)
            if n >= FIRST_OUTPUT_STEP:
                for number in range(2):
                    outputs[number] = output_tile(n, number, GRAD_BANKS[number])
            if half == 1:
                quantise_features_o(g)
            if_banks = transpose_dz(steps[n]["dz_if"])
            tanh_and_square(n + 1)
            if n >= FIRST_OUTPUT_STEP:
                for number in range(2):
                    store_output(n, number, outputs[number], s_copy)
            g0o_transposed(n + 1)
            g1_transposed(n + 1)
            tanh_back(n + 1)
            slope_o(n + 1)
            slope_f(n + 1)
            slope_i(n + 1)
            sigmoid(n + 2, "f")
            group_features(("if", n), "stage_if", if_banks, s_copy)

        n, g = STEPS - 2, GROUPS - 2
        last = steps[n + 1]
        sigmoid(n + 1, "o")
        gpsimd_products(n)
        psum_products(n)
        outputs[3] = output_tile(n - 1, 3, SPARE_BANKS[1])
        o_banks = transpose_dz(dz_o[g])
        outputs[2] = output_tile(n - 1, 2, SPARE_BANKS[0])
        o_tiles = [dr_tile(PASS_O, a, CELL_BANKS[a], range(g)) for a in range(2)]
        store_output(n - 1, 3, outputs[3], v_copy)
        group_features(("o", g), "stage_o", o_banks, s_copy)
        store_output(n - 1, 2, outputs[2], s_copy)
        if_banks = transpose_dz(steps[n]["dz_if"])
        o_tiles.extend([dr_tile(PASS_O, 2 + a, GRAD_BANKS[a], range(g)) for a in range(2)])
        last_ntc = three.tile([P, 4, HALF], F32, name="last_ntc", tag="a")
        last_sq = three.tile([P, 4, HALF], F32, name="last_sq", tag="i")
        nc.vector.tensor_tensor(out=last_ntc[:], in0=last["a"][:], in1=last["fc"][:], op=ALU.add)
        nc.scalar.activation(out=last_ntc[:], in_=last_ntc[:], func=ACT.Tanh, scale=-1.0)
        quantise_tokens(g, PASS_O, dz_o[g])
        quantise_tokens(g, 1, steps[n]["dz_if"])
        g0_times_o(n + 1, nc.vector, slice(GPSIMD_ROWS, 4))
        quantise_features_o(g)
        quantise_features_if(n - 1)
        group_features(("if", n), "stage_if", if_banks, s_copy)
        nc.scalar.activation(out=last_sq[:], in_=last_ntc[:], func=ACT.Square)
        for a in range(4):
            dr_passes(PASS_O, a, o_tiles[a], (g,))
        if_tiles = [dr_tile(1, a, SPARE_BANKS[a], range(g + 1)) for a in range(2)]

        n, g = STEPS - 1, GROUPS - 1
        slope_o(n)
        slope_i(n)
        rounded_product(dz_o[g], 64, 64, last_ntc[:], last["o"][:])
        quantise_features_if(n - 1)
        dh_before = [dh_tile(g - 1, j, DZT_BANKS[j]) for j in range(2)]
        quantise_tokens(g, PASS_O, dz_o[g])
        for a in range(4):
            dr_passes(PASS_O, a, o_tiles[a], (g,))
        for j in range(2):
            store_dh_tile(g - 1, j, dh_before[j], s_copy)
        o_banks = transpose_dz(dz_o[g])
        for a in range(4):
            store_dr_tile(PASS_O, a, o_tiles[a], s_copy)
        dh_before.extend([dh_tile(g - 1, 2 + e, CELL_BANKS[e]) for e in range(2)])
        if_tiles.extend([dr_tile(1, 2 + a, GRAD_BANKS[a], range(g)) for a in range(2)])
        group_features(("o", g), "stage_o", o_banks, s_copy)
        last_ndc = last["g0o"]
        minus_one_times(last_ndc[:], last_sq[:], last["g0o"][:])
        slope_f(n)
        nc.vector.tensor_tensor(out=last_ndc[:], in0=last_ndc[:], in1=last["g1"][:], op=ALU.subtract)
        last_dz_if = two.tile([P, 2048], BF16, name="dz_if", tag="dz_if", align_bytes=64)
        for gate, slope in enumerate(("a", "fc")):
            rounded_product(last_dz_if, 64 * gate, 64, last[slope][:], last_ndc[:])
        if_banks = transpose_dz(last_dz_if)
        for j in range(2, 4):
            store_dh_tile(g - 1, j, dh_before[j], s_copy)
        quantise_features_o(g)
        quantise_tokens(g, 1, last_dz_if)
        for a in range(4):
            dr_passes(1, a, if_tiles[a], (g,))
        group_features(("if", n), "stage_if", if_banks, v_copy)
        quantise_features_if(n)
        dh_banks = [bank(number) for number in CELL_BANKS + DZT_BANKS]
        for pair in range(2):
            for k_passes in ((0, PASS_O), (1,)):
                for j in (2 * pair, 2 * pair + 1):
                    dh_passes(g, j, dh_banks[j], k_passes)
        for a, copy in enumerate((s_copy, s_copy, v_copy, s_copy)):
            store_dr_tile(1, a, if_tiles[a], copy)
        for j, copy in enumerate((v_copy, s_copy, v_copy, s_copy)):
            store_dh_tile(g, j, dh_banks[j], copy)
